import numpy as np
import ml_dtypes


def mxq(x, axis, fmt="e4m3"):
    dtype, down = {"e4m3": (ml_dtypes.float8_e4m3fn, 7), "e5m2": (ml_dtypes.float8_e5m2, 14)}[fmt]
    v = np.moveaxis(np.asarray(x, np.float32).astype(ml_dtypes.bfloat16).astype(np.float64), axis, -1)
    blocks = v.reshape(v.shape[:-1] + (-1, 32))
    amax = np.abs(blocks).max(-1, keepdims=True)
    byte = np.maximum(np.where(amax > 0, np.frexp(amax)[1] - 1 + 127, 0) - down, 1)
    scale = np.exp2(byte - 127.0)
    codes = (blocks / scale).astype(np.float32).astype(dtype).astype(np.float64)
    return np.moveaxis((codes * scale).reshape(v.shape), -1, axis)


WIDE = False


def mx_kscale(k):
    if not WIDE:
        return np.ones(k)
    levels = np.array([18, -18])
    if k % 512:
        return np.exp2(np.random.permutation(np.resize(levels, k // 32))).repeat(32)
    a = np.empty((k // 512, 16))
    for p in range(k // 512):
        a[p, :8] = np.random.permutation(np.resize(levels, 8))
        for g in range(8):
            far = levels[np.abs(levels - a[p, g]) >= 10]
            a[p, g + 8] = far[np.random.randint(len(far))]
    return np.exp2(a.ravel()).repeat(32)


BF16 = ml_dtypes.bfloat16


def bf(x):
    return np.asarray(x, np.float32).astype(BF16)


def f64(x):
    return np.asarray(x).astype(np.float64)


B, C, H, W, S, HID, OC = 2, 128, 64, 64, 2, 1024, 512
H2, W2 = H // S, W // S
K1 = C * S * S
T = B * H2 * W2
N = OC // C
RESIDUAL = True


def sigmoid(a):
    return 1.0 / (1.0 + np.exp(-a))


def patchify(x):
    p = x.reshape(B, C, H2, S, W2, S)
    return p.transpose(0, 2, 4, 1, 3, 5).reshape(T, K1)


def unpatchify(p):
    p = p.reshape(B, H2, W2, C, S, S)
    return p.transpose(0, 3, 1, 4, 2, 5).reshape(B, C, H, W)


def setup_inputs():
    s = mx_kscale(T)
    u = mx_kscale(OC)
    u = u / u.max()
    v = mx_kscale(HID)
    sx = np.broadcast_to(s.reshape(B, 1, H2, 1, W2, 1), (B, C, H2, S, W2, S)).reshape(B, C, H, W)
    sg = s.reshape(B, 1, H2, W2)
    x0 = bf(np.random.standard_normal((B, C, H, W)))
    w1_0 = bf(np.random.standard_normal((HID, K1)) / np.sqrt(K1))
    bias1 = bf(np.random.standard_normal(HID) * 0.2)
    w2_0 = bf(np.random.standard_normal((OC, HID)) * 1.5 / np.sqrt(HID))
    bias2 = bf(np.random.standard_normal(OC) * 0.2)
    g = bf(np.random.standard_normal((B, OC, H2, W2)) * np.exp2(np.random.randint(-6, 1, (B, 1, H2, W2))) / sg * u.reshape(1, OC, 1, 1))
    o1 = patchify(f64(x0)) @ f64(w1_0).T + f64(bias1)
    return {"x": bf(f64(x0) * sx),
            "weight1": bf(f64(w1_0) / v[:, None]),
            "bias1": bias1,
            "weight2": bf(f64(w2_0) * v[None, :] / u[:, None]),
            "bias2": bias2,
            "o1": np.asarray(o1, np.float32),
            "grad_out": g}


def reference(x, weight1, bias1, weight2, bias2, o1, grad_out):
    go = f64(grad_out)
    g2 = go.transpose(0, 2, 3, 1).reshape(T, OC)
    dh = mxq(g2, 1, "e5m2") @ mxq(f64(weight2), 0, "e4m3")
    of = f64(o1)
    sg = sigmoid(of)
    dz1 = dh * (sg * (1.0 + of * (1.0 - sg)))
    dp = mxq(dz1, 1, "e5m2") @ mxq(f64(weight1), 0, "e4m3")
    dx = unpatchify(dp)
    if RESIDUAL:
        gp = go.reshape(B, C, N, H2, W2).sum(axis=2) / (S * S)
        gp = np.broadcast_to(gp[:, :, :, None, :, None], (B, C, H2, S, W2, S)).reshape(B, C, H, W)
        dx = dx + gp
    p = patchify(f64(x))
    dw1 = mxq(dz1, 0, "e5m2").T @ mxq(p, 0, "e4m3")
    return dx, dw1

@@ -1,0 +1,363 @@
+from contextlib import ExitStack
+
+import concourse.mybir as mybir
+from concourse.masks import make_identity
+
+B, C, H, W = 2, 128, 64, 64
+HID, OC, K1 = 1024, 512, 512
+T = 2048
+P = 128
+F32 = mybir.dt.float32
+BF16 = mybir.dt.bfloat16
+U32 = mybir.dt.uint32
+U8 = mybir.dt.uint8
+E4 = mybir.dt.float8_e4m3fn_x4
+E5 = mybir.dt.float8_e5m2_x4
+ALU = mybir.AluOpType
+ACT = mybir.ActivationFunctionType
+FLOPS = 3 * 2 * T * HID * 512
+BYTES = 2 * (B * C * H * W + HID * K1 + OC * HID + T * OC) + 4 * (T * HID + B * C * H * W + HID * K1)
+G = 4
+NU = 8
+
+
+def tile_memoryefficientpatchdownscale_v_kernel(
+    tc, x, weight1, bias1, weight2, bias2, o1, grad_out, out_0, out_1
+):
+    nc = tc.nc
+    go = grad_out.rearrange("b (p j) y w -> b p j (y w)", j=4)
+    w2v = weight2.rearrange("(p j) h -> p j h", j=4)
+    w1v = weight1.rearrange("(f p j) k -> f p j k", p=P, j=4)
+    o1v = o1.rearrange("(g p j) h -> g p j h", p=P, j=4)
+    xv = x.rearrange("b c (s r) w -> b s c (r w)", s=2)
+    o0v = out_0.rearrange("b c (s r) w -> b s c (r w)", s=2)
+    o1o = out_1.rearrange("(f t m) k -> f t m k", m=P, t=4)
+
+    with ExitStack() as ctx:
+        keep = ctx.enter_context(tc.tile_pool(name="keep", bufs=1))
+        rot = ctx.enter_context(tc.tile_pool(name="rot", bufs=2))
+        psum = ctx.enter_context(tc.psum_pool(name="psum", bufs=2))
+
+        warm = keep.tile([P, 1], F32, name="warm")
+        idf = keep.tile([P, P], F32, name="idf")
+        idb = keep.tile([P, P], BF16, name="idb")
+        g_c = keep.tile([P, T], U32, name="g_c", align_bytes=64)
+        g_s = keep.tile([P, T], U8, name="g_s", align_bytes=64)
+        w2_c = keep.tile([P, HID], U32, name="w2_c", align_bytes=64)
+        w2_s = keep.tile([P, HID], U8, name="w2_s", align_bytes=64)
+        w1_c = keep.tile([P, 2 * K1], U32, name="w1_c", align_bytes=64)
+        w1_s = keep.tile([P, 2 * K1], U8, name="w1_s", align_bytes=64)
+        p_c = keep.tile([P, G * 512], U32, name="p_c", align_bytes=64)
+        p_s = keep.tile([P, G * 512], U8, name="p_s", align_bytes=64)
+        tok_c = keep.tile([P, G * HID], U32, name="tok_c", align_bytes=64)
+        tok_s = keep.tile([P, G * HID], U8, name="tok_s", align_bytes=64)
+        hid_c = keep.tile([P, 2 * T], U32, name="hid_c", align_bytes=64)
+        hid_s = keep.tile([P, 2 * T], U8, name="hid_s", align_bytes=64)
+        pooled = keep.tile([P, T], F32, name="pooled")
+
+        nc.vector.memset(warm[:], 0.0)
+        make_identity(nc, idf[:])
+        make_identity(nc, idb[:])
+
+        graw, wraw, xraw, o1t, rt, dzi, xsb = {}, {}, {}, {}, {}, {}, {}
+        mixed, hidi, dhb, trb, stg, o0t = {}, {}, {}, {}, {}, {}
+
+        def load_g(g):
+            graw[g] = rot.tile([P, 4, 512], BF16, name="graw", tag="graw", bufs=4)
+            b, s = divmod(g, 2)
+            nc.sync.dma_start(out=graw[g][:], in_=go[b, :, :, s * 512 : (s + 1) * 512])
+
+        def load_w(which, f):
+            wraw[which, f] = rot.tile([P, 4, 512], BF16, name="wraw", tag="wraw", bufs=3)
+            src = w2v[:, :, f * 512 : (f + 1) * 512] if which == 2 else w1v[f]
+            nc.sync.dma_start(out=wraw[which, f][:], in_=src)
+
+        def load_x(g):
+            xraw[g] = rot.tile([P, 2048], BF16, name="xraw", tag="xraw", bufs=2)
+            b, s = divmod(g, 2)
+            nc.sync.dma_start(out=xraw[g][:], in_=xv[b, s])
+
+        def load_o1(n):
+            f, g = divmod(n, G)
+            o1t[n] = rot.tile([P, 4, 512], F32, name="o1t", tag="o1t", bufs=4)
+            for j in (0, 2):
+                nc.sync.dma_start(
+                    out=o1t[n][:, j : j + 2, :], in_=o1v[g, :, j : j + 2, f * 512 : (f + 1) * 512]
+                )
+
+        def mix_tile(key):
+            mixed[key] = rot.tile([P, 2048], BF16, name="mix", tag="mix", bufs=3, align_bytes=64)
+            return mixed[key]
+
+        def mix_g(g):
+            d = mix_tile(("g", g))
+            nc.vector.tensor_copy(
+                out=d[:].rearrange("p (t m j) -> p m j t", t=4, j=4),
+                in_=graw[g][:].rearrange("p j (m t) -> p m j t", t=4),
+            )
+
+        def mix_w2(f):
+            d = mix_tile(("w2", f))
+            nc.vector.tensor_scalar(
+                out=d[:].rearrange("p (m t j) -> p m j t", t=4, j=4),
+                in0=wraw[2, f][:].rearrange("p j (m t) -> p m j t", t=4),
+                scalar1=-0.5,
+                scalar2=None,
+                op0=ALU.mult,
+            )
+
+        def mix_w1(f):
+            d = mix_tile(("w1", f))
+            nc.scalar.copy(
+                out=d[:].rearrange("p (t m j) -> p m j t", t=4, j=4),
+                in_=wraw[1, f][:].rearrange("p j (m t) -> p m j t", t=4),
+            )
+
+        def quant(src, codes, scales, c0, fmt):
+            nc.vector.quantize_mx(
+                out=codes[:, c0 : c0 + 512].bitcast(fmt), scales=scales[:, c0 : c0 + 512], in_=src[:]
+            )
+
+        def q_g(g):
+            quant(mixed["g", g], g_c, g_s, g * 512, E5)
+
+        def q_w2(f):
+            quant(mixed["w2", f], w2_c, w2_s, f * 512, E4)
+
+        def q_w1(f):
+            quant(mixed["w1", f], w1_c, w1_s, f * 512, E4)
+
+        def q_p(g):
+            quant(mixed["p", g], p_c, p_s, g * 512, E4)
+
+        def q_tok(n):
+            f, g = divmod(n, G)
+            quant(dzi[n], tok_c, tok_s, g * HID + f * 512, E5)
+
+        def q_hid(n):
+            quant(hidi[n], hid_c, hid_s, n * 512, E5)
+
+        def mx(out, lc, ls, l0, lf, rc, rs, r0, rf, start, stop):
+            nc.tensor.matmul_mx(
+                out=out[:],
+                lhsT=lc[:, l0 : l0 + 128].bitcast(lf),
+                lhsT_scale=ls[:, l0 : l0 + 128],
+                rhs=rc[:, r0 : r0 + 512].bitcast(rf),
+                rhs_scale=rs[:, r0 : r0 + 512],
+                start=start,
+                stop=stop,
+            )
+
+        def dh(n):
+            f, g = divmod(n, G)
+            for j in range(4):
+                dhb[n, j] = psum.tile([P, 512], F32, name="dh", tag="dh", bufs=4)
+                mx(dhb[n, j], g_c, g_s, g * 512 + j * 128, E5, w2_c, w2_s, f * 512, E4, True, True)
+
+        def silu(n):
+            rt[n] = rot.tile([P, 4, 512], F32, name="rt", tag="rt", bufs=2)
+            for j in (0, 2):
+                nc.scalar.activation(
+                    out=rt[n][:, j : j + 2, :], in_=o1t[n][:, j : j + 2, :], func=ACT.Silu, scale=-1.0
+                )
+
+        def tanh(n):
+            for j in (0, 2):
+                nc.scalar.activation(
+                    out=o1t[n][:, j : j + 2, :], in_=o1t[n][:, j : j + 2, :], func=ACT.Tanh, scale=0.5
+                )
+
+        def d1(n):
+            for j in range(4):
+                nc.vector.scalar_tensor_tensor(
+                    out=rt[n][:, j, :],
+                    in0=rt[n][:, j, :],
+                    scalar=1.0,
+                    in1=dhb[n, j][:],
+                    op0=ALU.subtract,
+                    op1=ALU.mult,
+                )
+
+        def d2(n):
+            dzi[n] = rot.tile([P, 2048], BF16, name="dzi", tag="dzi", bufs=2, align_bytes=64)
+            nc.vector.scalar_tensor_tensor(
+                out=dzi[n][:].rearrange("p (h j) -> p h j", j=4),
+                in0=o1t[n][:].rearrange("p j h -> p h j"),
+                scalar=1.0,
+                in1=rt[n][:].rearrange("p j h -> p h j"),
+                op0=ALU.add,
+                op1=ALU.mult,
+            )
+
+        def tr(n):
+            words = dzi[n][:].bitcast(F32)
+            for u in range(2):
+                bank = psum.tile([P, 4, P], F32, name="tr", tag="tr", bufs=2)
+                trb[n, u] = bank
+                for t in range(4):
+                    nc.tensor.transpose(bank[:, t, :], words[:, 2 * t + u : 1024 : 8], idf[:])
+
+        def cp_tr(n):
+            hidi[n] = rot.tile([P, 2048], BF16, name="hidi", tag="hidi", bufs=2, align_bytes=64)
+            for u in range(2):
+                nc.scalar.copy(
+                    out=hidi[n][:, 1024 * u : 1024 * (u + 1)].rearrange("m (c t) -> m c t", t=4),
+                    in_=trb[n, u][:].rearrange("m t p -> m (t p)").bitcast(BF16).rearrange("m (t c) -> m c t", t=4),
+                )
+
+        def sort_x(g):
+            xsb[g] = rot.tile([P, 2, 4, P], F32, name="xs", tag="xs", bufs=1)
+            words = xraw[g][:].bitcast(F32).rearrange("c (i u j t) -> c u i j t", i=16, u=2, t=4)
+            for u in range(2):
+                nc.vector.tensor_copy(
+                    out=xsb[g][:, u, :, :].rearrange("c t (i j) -> c i j t", i=16), in_=words[:, u]
+                )
+
+        def tr_x(g):
+            for u in range(2):
+                bank = psum.tile([P, 4, P], F32, name="tr", tag="tr", bufs=2)
+                trb["x", g, u] = bank
+                for t in range(4):
+                    nc.tensor.transpose(bank[:, t, :], xsb[g][:, u, t, :], idf[:])
+
+        def cp_x(g):
+            d = mix_tile(("p", g))
+            for u in range(2):
+                nc.scalar.copy(
+                    out=d[:, 1024 * u : 1024 * (u + 1)].rearrange("m (c t) -> m c t", t=4),
+                    in_=trb["x", g, u][:].rearrange("m t p -> m (t p)").bitcast(BF16).rearrange("m (t c) -> m c t", t=4),
+                )
+
+        def pool_mm(g):
+            bank = psum.tile([P, 512], F32, name="acc", tag="acc", bufs=2)
+            for j in range(4):
+                nc.tensor.matmul(bank[:], lhsT=idb[:], rhs=graw[g][:, j, :], start=(j == 0), stop=(j == 3))
+            nc.scalar.copy(out=pooled[:, g * 512 : (g + 1) * 512], in_=bank[:])
+
+        def dp(g):
+            o0t[g] = rot.tile([P, 2048], F32, name="o0t", tag="o0t", bufs=2)
+            for u in range(2):
+                stg[g, u] = rot.tile([P, 2, 512], F32, name="stg", tag="stg", bufs=3)
+                for v in range(2):
+                    q = 2 * u + v
+                    bank = psum.tile([P, 512], F32, name="acc", tag="acc", bufs=2)
+                    for f in range(2):
+                        mx(bank, w1_c, w1_s, f * 512 + q * 128, E4, hid_c, hid_s, f * T + g * 512, E5, f == 0, f == 1)
+                    nc.scalar.copy(
+                        out=stg[g, u][:, v, :].rearrange("c (p u e) -> c p u e", u=2, e=2),
+                        in_=bank[:].rearrange("c (u p e) -> c p u e", u=2, e=2),
+                    )
+
+        def add(g):
+            b, s = divmod(g, 2)
+            for u in range(2):
+                pl = pooled[:, g * 512 : (g + 1) * 512].rearrange("c (i j) -> c i j", i=16)
+                nc.vector.scalar_tensor_tensor(
+                    out=o0t[g][:].rearrange("c (i u j v) -> c u i j v", i=16, u=2, v=2)[:, u],
+                    in0=pl.unsqueeze(3).to_broadcast([P, 16, 32, 2]),
+                    scalar=0.25,
+                    in1=stg[g, u][:].rearrange("c v (i j) -> c i j v", i=16),
+                    op0=ALU.mult,
+                    op1=ALU.add,
+                )
+            nc.sync.dma_start(out=o0v[b, s], in_=o0t[g][:])
+
+        def dw1(f, t, tag, on_vector):
+            bufs = 4 if tag == "dh" else 2
+            bank = psum.tile([P, 512], F32, name=tag, tag=tag, bufs=bufs)
+            for g in range(G):
+                mx(bank, tok_c, tok_s, g * HID + f * 512 + t * 128, E5, p_c, p_s, g * 512, E4, g == 0, g == 3)
+            res = rot.tile([P, 512], F32, name="res", tag="res", bufs=4)
+            dst = res[:].rearrange("m (c u v) -> m c u v", u=2, v=2)
+            src = bank[:].rearrange("m (u c v) -> m c u v", u=2, v=2)
+            if on_vector:
+                nc.vector.tensor_copy(out=dst, in_=src)
+            else:
+                nc.scalar.copy(out=dst, in_=src)
+            nc.sync.dma_start(out=o1o[f, t], in_=res[:])
+
+        with tc.manual_schedule():
+            load_g(0)
+            load_w(2, 0)
+            load_o1(0)
+            load_g(1)
+            load_o1(1)
+            load_g(2)
+            load_x(0)
+            load_o1(2)
+            load_w(2, 1)
+            load_g(3)
+            load_x(1)
+            load_o1(3)
+
+            nc.scalar.activation(out=warm[:], in_=warm[:], func=ACT.Silu, scale=-1.0)
+            mix_g(0)
+            mix_w2(0)
+            q_g(0)
+            q_w2(0)
+            dh(0)
+            silu(0)
+            tanh(0)
+            mix_g(1)
+            q_g(1)
+
+            for n in range(NU):
+                f, g = divmod(n, G)
+                if n > 0:
+                    cp_tr(n - 1)
+                d1(n)
+                if n + 1 < NU:
+                    dh(n + 1)
+                    silu(n + 1)
+                if f == 0:
+                    sort_x(n)
+                    pool_mm(n)
+                    tr_x(n)
+                    cp_x(n)
+                if n > 0:
+                    q_hid(n - 1)
+                if n >= 5:
+                    dp(n - 5)
+                d2(n)
+                if n + 1 < NU:
+                    tanh(n + 1)
+                if n + 2 < G:
+                    mix_g(n + 2)
+                tr(n)
+                if n + 4 < NU:
+                    load_o1(n + 4)
+                if n == 0:
+                    load_x(2)
+                    load_w(1, 0)
+                if n == 1:
+                    load_x(3)
+                    load_w(1, 1)
+                if n == 2:
+                    mix_w2(1)
+                if n == 3:
+                    mix_w1(0)
+                q_tok(n)
+                if n + 2 < G:
+                    q_g(n + 2)
+                if n == 2:
+                    q_w2(1)
+                if f == 0:
+                    q_p(n)
+                if n == 3:
+                    mix_w1(1)
+                    q_w1(0)
+                if n == 4:
+                    q_w1(1)
+                if n >= 5:
+                    add(n - 5)
+                if n == 4 or n == 5:
+                    dw1(0, 2 * (n - 4), "acc", False)
+                    dw1(0, 2 * (n - 4) + 1, "acc", False)
+            dw1(1, 0, "dh", False)
+            dw1(1, 1, "dh", True)
+            cp_tr(NU - 1)
+            q_hid(NU - 1)
+            dp(3)
+            dw1(1, 2, "dh", True)
+            dw1(1, 3, "dh", True)
+            add(3)

@@ -18,6 +18,9 @@ ACT = mybir.ActivationFunctionType
 FLOPS = 3 * 2 * T * HID * 512
 BYTES = 2 * (B * C * H * W + HID * K1 + OC * HID + T * OC) + 4 * (T * HID + B * C * H * W + HID * K1)
 G = 4
+UNITS = ((0, 0), (0, 1), (1, 0), (0, 2), (1, 1), (0, 3), (1, 2), (1, 3))
+ZG = (0, 1)
+BUFS = {"dh": 4, "tr": 2, "acc": 2}
 NU = 8
 
 
@@ -41,6 +44,7 @@ def tile_memoryefficientpatchdownscale_v_kernel(
         warm = keep.tile([P, 1], F32, name="warm")
         idf = keep.tile([P, P], F32, name="idf")
         idb = keep.tile([P, P], BF16, name="idb")
+        idn = keep.tile([P, P], BF16, name="idn")
         g_c = keep.tile([P, T], U32, name="g_c", align_bytes=64)
         g_s = keep.tile([P, T], U8, name="g_s", align_bytes=64)
         w2_c = keep.tile([P, HID], U32, name="w2_c", align_bytes=64)
@@ -51,16 +55,20 @@ def tile_memoryefficientpatchdownscale_v_kernel(
         p_s = keep.tile([P, G * 512], U8, name="p_s", align_bytes=64)
         tok_c = keep.tile([P, G * HID], U32, name="tok_c", align_bytes=64)
         tok_s = keep.tile([P, G * HID], U8, name="tok_s", align_bytes=64)
-        hid_c = keep.tile([P, 2 * T], U32, name="hid_c", align_bytes=64)
-        hid_s = keep.tile([P, 2 * T], U8, name="hid_s", align_bytes=64)
+        hid_c = keep.tile([P, 6 * 1280], U32, name="hid_c", align_bytes=64)
+        hid_s = keep.tile([P, 6 * 1280], U8, name="hid_s", align_bytes=64)
         pooled = keep.tile([P, T], F32, name="pooled")
 
         nc.vector.memset(warm[:], 0.0)
         make_identity(nc, idf[:])
         make_identity(nc, idb[:])
+        nc.vector.tensor_scalar(out=idn[:], in0=idb[:], scalar1=-0.5, scalar2=None, op0=ALU.mult)
+        for part in (hid_c[:], hid_s[:].bitcast(U32)):
+            for z in (0, 2, 4):
+                nc.gpsimd.memset(part.rearrange("p (s d w) -> p d s w", s=6, d=5)[:, z], 0)
 
         graw, wraw, xraw, o1t, rt, dzi, xsb = {}, {}, {}, {}, {}, {}, {}
-        mixed, hidi, dhb, trb, stg, o0t = {}, {}, {}, {}, {}, {}
+        mixed, hidi, dhb, trb, accb, stg = {}, {}, {}, {}, {}, {}
 
         def load_g(g):
             graw[g] = rot.tile([P, 4, 512], BF16, name="graw", tag="graw", bufs=4)
@@ -78,7 +86,7 @@ def tile_memoryefficientpatchdownscale_v_kernel(
             nc.sync.dma_start(out=xraw[g][:], in_=xv[b, s])
 
         def load_o1(n):
-            f, g = divmod(n, G)
+            f, g = UNITS[n]
             o1t[n] = rot.tile([P, 4, 512], F32, name="o1t", tag="o1t", bufs=4)
             for j in (0, 2):
                 nc.sync.dma_start(
@@ -86,7 +94,7 @@ def tile_memoryefficientpatchdownscale_v_kernel(
                 )
 
         def mix_tile(key):
-            mixed[key] = rot.tile([P, 2048], BF16, name="mix", tag="mix", bufs=3, align_bytes=64)
+            mixed[key] = rot.tile([P, 2048], BF16, name="mix", tag="mix", bufs=2, align_bytes=64)
             return mixed[key]
 
         def mix_g(g):
@@ -98,20 +106,37 @@ def tile_memoryefficientpatchdownscale_v_kernel(
 
         def mix_w2(f):
             d = mix_tile(("w2", f))
-            nc.vector.tensor_scalar(
+            nc.scalar.mul(
                 out=d[:].rearrange("p (m t j) -> p m j t", t=4, j=4),
-                in0=wraw[2, f][:].rearrange("p j (m t) -> p m j t", t=4),
-                scalar1=-0.5,
-                scalar2=None,
-                op0=ALU.mult,
+                in_=wraw[2, f][:].rearrange("p j (m t) -> p m j t", t=4),
+                mul=-0.5,
             )
 
-        def mix_w1(f):
-            d = mix_tile(("w1", f))
-            nc.scalar.copy(
-                out=d[:].rearrange("p (t m j) -> p m j t", t=4, j=4),
-                in_=wraw[1, f][:].rearrange("p j (m t) -> p m j t", t=4),
-            )
+        def move(raw, ident, h):
+            bank = psum.tile([P, 4, 256], BF16, name="acc", tag="acc", bufs=BUFS["acc"])
+            for j in range(4):
+                nc.tensor.matmul(
+                    bank[:, j, :], lhsT=ident[:], rhs=raw[:, j, h * 256 : h * 256 + 256], start=True, stop=True
+                )
+            return bank
+
+        def pe_mix_w2(f):
+            d = mix_tile(("w2", f))
+            for h in range(2):
+                bank = move(wraw[2, f], idn, h)
+                nc.scalar.copy(
+                    out=d[:, h * 1024 : h * 1024 + 1024].rearrange("p (c j) -> p c j", j=4),
+                    in_=bank[:].rearrange("p j c -> p c j"),
+                )
+
+        def pe_mix(raw, key):
+            d = mix_tile(key)
+            for h in range(2):
+                bank = move(raw, idb, h)
+                nc.scalar.copy(
+                    out=d[:].rearrange("p (t m j) -> p t m j", t=4, j=4)[:, :, h * 64 : h * 64 + 64, :],
+                    in_=bank[:].rearrange("p j (m t) -> p t m j", t=4),
+                )
 
         def quant(src, codes, scales, c0, fmt):
             nc.vector.quantize_mx(
@@ -131,11 +156,19 @@ def tile_memoryefficientpatchdownscale_v_kernel(
             quant(mixed["p", g], p_c, p_s, g * 512, E4)
 
         def q_tok(n):
-            f, g = divmod(n, G)
+            f, g = UNITS[n]
             quant(dzi[n], tok_c, tok_s, g * HID + f * 512, E5)
 
+        def slot(f, g):
+            return 1280 * (g if f == 0 else 4 + g % 2)
+
         def q_hid(n):
-            quant(hidi[n], hid_c, hid_s, n * 512, E5)
+            f, g = UNITS[n]
+            c0 = slot(f, g) + 256
+            cuts = ((0, 1024, 0), (1024, 2048, 512)) if g in ZG else ((0, 2048, 0),)
+            for a, b, d in cuts:
+                c = slice(c0 + d, c0 + d + (b - a) // 4)
+                nc.vector.quantize_mx(out=hid_c[:, c].bitcast(E5), scales=hid_s[:, c], in_=hidi[n][:, a:b])
 
         def mx(out, lc, ls, l0, lf, rc, rs, r0, rf, start, stop):
             nc.tensor.matmul_mx(
@@ -149,7 +182,7 @@ def tile_memoryefficientpatchdownscale_v_kernel(
             )
 
         def dh(n):
-            f, g = divmod(n, G)
+            f, g = UNITS[n]
             for j in range(4):
                 dhb[n, j] = psum.tile([P, 512], F32, name="dh", tag="dh", bufs=4)
                 mx(dhb[n, j], g_c, g_s, g * 512 + j * 128, E5, w2_c, w2_s, f * 512, E4, True, True)
@@ -201,8 +234,8 @@ def tile_memoryefficientpatchdownscale_v_kernel(
             hidi[n] = rot.tile([P, 2048], BF16, name="hidi", tag="hidi", bufs=2, align_bytes=64)
             for u in range(2):
                 nc.scalar.copy(
-                    out=hidi[n][:, 1024 * u : 1024 * (u + 1)].rearrange("m (c t) -> m c t", t=4),
-                    in_=trb[n, u][:].rearrange("m t p -> m (t p)").bitcast(BF16).rearrange("m (t c) -> m c t", t=4),
+                    out=hidi[n][:].rearrange("m (p u e t) -> m u p e t", u=2, e=2, t=4)[:, u],
+                    in_=trb[n, u][:].rearrange("m t p -> m (t p)").bitcast(BF16).rearrange("m (t p e) -> m p e t", t=4, e=2),
                 )
 
         def sort_x(g):
@@ -229,47 +262,65 @@ def tile_memoryefficientpatchdownscale_v_kernel(
                 )
 
         def pool_mm(g):
-            bank = psum.tile([P, 512], F32, name="acc", tag="acc", bufs=2)
+            accb["p", g] = psum.tile([P, 512], F32, name="acc", tag="acc", bufs=2)
             for j in range(4):
-                nc.tensor.matmul(bank[:], lhsT=idb[:], rhs=graw[g][:, j, :], start=(j == 0), stop=(j == 3))
-            nc.scalar.copy(out=pooled[:, g * 512 : (g + 1) * 512], in_=bank[:])
-
-        def dp(g):
-            o0t[g] = rot.tile([P, 2048], F32, name="o0t", tag="o0t", bufs=2)
-            for u in range(2):
-                stg[g, u] = rot.tile([P, 2, 512], F32, name="stg", tag="stg", bufs=3)
-                for v in range(2):
-                    q = 2 * u + v
-                    bank = psum.tile([P, 512], F32, name="acc", tag="acc", bufs=2)
-                    for f in range(2):
-                        mx(bank, w1_c, w1_s, f * 512 + q * 128, E4, hid_c, hid_s, f * T + g * 512, E5, f == 0, f == 1)
-                    nc.scalar.copy(
-                        out=stg[g, u][:, v, :].rearrange("c (p u e) -> c p u e", u=2, e=2),
-                        in_=bank[:].rearrange("c (u p e) -> c p u e", u=2, e=2),
-                    )
-
-        def add(g):
-            b, s = divmod(g, 2)
-            for u in range(2):
-                pl = pooled[:, g * 512 : (g + 1) * 512].rearrange("c (i j) -> c i j", i=16)
-                nc.vector.scalar_tensor_tensor(
-                    out=o0t[g][:].rearrange("c (i u j v) -> c u i j v", i=16, u=2, v=2)[:, u],
-                    in0=pl.unsqueeze(3).to_broadcast([P, 16, 32, 2]),
-                    scalar=0.25,
-                    in1=stg[g, u][:].rearrange("c v (i j) -> c i j v", i=16),
-                    op0=ALU.mult,
-                    op1=ALU.add,
+                nc.tensor.matmul(
+                    accb["p", g][:], lhsT=idb[:], rhs=graw[g][:, j, :], start=(j == 0), stop=(j == 3)
                 )
-            nc.sync.dma_start(out=o0v[b, s], in_=o0t[g][:])
 
-        def dw1(f, t, tag, on_vector):
-            bufs = 4 if tag == "dh" else 2
-            bank = psum.tile([P, 512], F32, name=tag, tag=tag, bufs=bufs)
-            for g in range(G):
-                mx(bank, tok_c, tok_s, g * HID + f * 512 + t * 128, E5, p_c, p_s, g * 512, E4, g == 0, g == 3)
-            res = rot.tile([P, 512], F32, name="res", tag="res", bufs=4)
+        def cp_pool(g):
+            nc.scalar.copy(out=pooled[:, g * 512 : (g + 1) * 512], in_=accb["p", g][:])
+
+        def dp(g, u, h, tag="acc"):
+            accb[g, u, h] = psum.tile([P, 512], F32, name=tag, tag=tag, bufs=BUFS[tag])
+            for f in range(2):
+                for v in range(2):
+                    c0 = slot(f, g) + 512 * h + 256 * (1 - v)
+                    mx(accb[g, u, h], w1_c, w1_s, f * 512 + (2 * u + v) * 128, E4, hid_c, hid_s, c0, E5, f + v == 0, f + v == 2)
+
+        def dps(g, q, tag="acc"):
+            accb[g, q] = psum.tile([P, 512], F32, name=tag, tag=tag, bufs=BUFS[tag])
+            for f in range(2):
+                mx(accb[g, q], w1_c, w1_s, f * 512 + q * 128, E4, hid_c, hid_s, slot(f, g) + 256, E5, f == 0, f == 1)
+
+        def stage(g, q, on_vector=False):
+            u, v = divmod(q, 2)
+            if v == 0:
+                stg[g, u] = rot.tile([P, 2, 512], F32, name="stg", tag="stg", bufs=2)
+            copy = nc.vector.tensor_copy if on_vector else nc.scalar.copy
+            copy(out=stg[g, u][:, v, :], in_=accb[g, q][:])
+
+        def add(g, u, h):
+            if (g, "o") not in accb:
+                accb[g, "o"] = rot.tile([P, 2048], F32, name="o0t", tag="o0t", bufs=2)
+            o = accb[g, "o"]
+            if g in ZG:
+                src = accb[g, u, h][:].rearrange("c (v t) -> c v t", v=2)
+            else:
+                src = stg[g, u][:, :, h * 256 : h * 256 + 256]
+            pl = pooled[:, g * 512 + h * 256 : g * 512 + h * 256 + 256]
+            nc.vector.scalar_tensor_tensor(
+                out=o[:, h * 1024 : h * 1024 + 1024].rearrange("c (i u j v) -> c u i j v", u=2, j=32, v=2)[:, u],
+                in0=pl.rearrange("c (i j) -> c i j", j=32).unsqueeze(3).to_broadcast([P, 8, 32, 2]),
+                scalar=0.25,
+                in1=src.rearrange("c v (i j) -> c i j v", j=32),
+                op0=ALU.mult,
+                op1=ALU.add,
+            )
+            if u == 1:
+                b, s = divmod(g, 2)
+                nc.sync.dma_start(out=o0v[b, s, :, h * 1024 : h * 1024 + 1024], in_=o[:, h * 1024 : h * 1024 + 1024])
+
+        def dw1(f, t, gs, tag):
+            if gs[0] == 0:
+                accb["w", f, t] = psum.tile([P, 512], F32, name=tag, tag=tag, bufs=BUFS[tag])
+            for g in gs:
+                mx(accb["w", f, t], tok_c, tok_s, g * HID + f * 512 + t * 128, E5, p_c, p_s, g * 512, E4, g == 0, g == 3)
+
+        def out1(f, t, on_vector):
+            res = rot.tile([P, 512], F32, name="res", tag="res", bufs=3)
             dst = res[:].rearrange("m (c u v) -> m c u v", u=2, v=2)
-            src = bank[:].rearrange("m (u c v) -> m c u v", u=2, v=2)
+            src = accb["w", f, t][:].rearrange("m (u c v) -> m c u v", u=2, v=2)
             if on_vector:
                 nc.vector.tensor_copy(out=dst, in_=src)
             else:
@@ -277,87 +328,136 @@ def tile_memoryefficientpatchdownscale_v_kernel(
             nc.sync.dma_start(out=o1o[f, t], in_=res[:])
 
         with tc.manual_schedule():
-            load_g(0)
             load_w(2, 0)
+            load_g(0)
             load_o1(0)
             load_g(1)
             load_o1(1)
-            load_g(2)
-            load_x(0)
-            load_o1(2)
             load_w(2, 1)
-            load_g(3)
-            load_x(1)
+            load_o1(2)
+            load_x(0)
+            load_g(2)
+            load_w(1, 0)
             load_o1(3)
+            load_x(1)
 
             nc.scalar.activation(out=warm[:], in_=warm[:], func=ACT.Silu, scale=-1.0)
-            mix_g(0)
             mix_w2(0)
+            mix_g(0)
             q_g(0)
             q_w2(0)
+            pool_mm(0)
             dh(0)
             silu(0)
-            tanh(0)
             mix_g(1)
-            q_g(1)
+            tanh(0)
+            cp_pool(0)
 
             for n in range(NU):
-                f, g = divmod(n, G)
+                f, g = UNITS[n]
+                last = n == NU - 1
                 if n > 0:
                     cp_tr(n - 1)
+                if n in (4, 6):
+                    dp(n // 2 - 2, 0, 0)
+                    dp(n // 2 - 2, 1, 0)
+                if last:
+                    for t in (2, 3):
+                        dw1(0, t, range(G), "acc")
+                        out1(0, t, False)
                 d1(n)
-                if n + 1 < NU:
+                if n == 0:
+                    q_g(1)
+                if n == 1:
+                    q_w2(1)
+                if n == 2:
+                    q_g(2)
+                if n == 3:
+                    q_w1(0)
+                    q_w1(1)
+                if n == 4:
+                    q_g(3)
+                if not last:
                     dh(n + 1)
                     silu(n + 1)
-                if f == 0:
-                    sort_x(n)
-                    pool_mm(n)
-                    tr_x(n)
-                    cp_x(n)
-                if n > 0:
+                else:
                     q_hid(n - 1)
-                if n >= 5:
-                    dp(n - 5)
+                    for q in range(2):
+                        dps(2, q)
+                        stage(2, q)
+                    for t in range(2):
+                        dw1(1, t, range(3), "dh")
+                if n in (4, 6):
+                    gz = n // 2 - 2
+                    add(gz, 0, 0)
+                    add(gz, 1, 0)
+                    dp(gz, 0, 1)
+                    dp(gz, 1, 1)
+                if 2 <= n <= 5:
+                    tr_x(n - 2)
+                    cp_x(n - 2)
                 d2(n)
-                if n + 1 < NU:
+                if not last:
                     tanh(n + 1)
-                if n + 2 < G:
-                    mix_g(n + 2)
                 tr(n)
                 if n + 4 < NU:
                     load_o1(n + 4)
                 if n == 0:
-                    load_x(2)
-                    load_w(1, 0)
-                if n == 1:
-                    load_x(3)
+                    load_g(3)
                     load_w(1, 1)
+                if n in (1, 2):
+                    load_x(n + 1)
+                if n in (0, 2, 4):
+                    gg = n // 2 + 1
+                    pool_mm(gg)
+                    cp_pool(gg)
+                if n == 0:
+                    pe_mix_w2(1)
+                if n == 1:
+                    mix_g(2)
+                    pe_mix(wraw[1, 0], ("w1", 0))
                 if n == 2:
-                    mix_w2(1)
+                    pe_mix(wraw[1, 1], ("w1", 1))
                 if n == 3:
-                    mix_w1(0)
+                    pe_mix(graw[3], ("g", 3))
+                if 0 < n and not last:
+                    q_hid(n - 1)
+                if 1 <= n <= G:
+                    sort_x(n - 1)
+                if last:
+                    for q in (2, 3):
+                        dps(2, q)
+                        stage(2, q)
+                    cp_tr(n)
                 q_tok(n)
-                if n + 2 < G:
-                    q_g(n + 2)
-                if n == 2:
-                    q_w2(1)
-                if f == 0:
-                    q_p(n)
-                if n == 3:
-                    mix_w1(1)
-                    q_w1(0)
-                if n == 4:
-                    q_w1(1)
-                if n >= 5:
-                    add(n - 5)
-                if n == 4 or n == 5:
-                    dw1(0, 2 * (n - 4), "acc", False)
-                    dw1(0, 2 * (n - 4) + 1, "acc", False)
-            dw1(1, 0, "dh", False)
-            dw1(1, 1, "dh", True)
-            cp_tr(NU - 1)
+                if 2 <= n <= 5:
+                    q_p(n - 2)
+                if n in (4, 6):
+                    add(gz, 0, 1)
+                    add(gz, 1, 1)
+                if n == 6:
+                    for t in (0, 1):
+                        dw1(0, t, range(G), "acc")
+                        out1(0, t, False)
+            add(2, 0, 0)
+            add(2, 1, 0)
             q_hid(NU - 1)
-            dp(3)
-            dw1(1, 2, "dh", True)
-            dw1(1, 3, "dh", True)
-            add(3)
+            add(2, 0, 1)
+            add(2, 1, 1)
+            for t in range(2):
+                dw1(1, t, [3], "dh")
+            dps(3, 0)
+            dps(3, 1)
+            dps(3, 2, "tr")
+            dps(3, 3, "tr")
+            out1(1, 0, False)
+            out1(1, 1, True)
+            for q in range(4):
+                stage(3, q, q % 2 == 1)
+            for t in (2, 3):
+                dw1(1, t, range(G), "dh")
+            for h in range(2):
+                for u in range(2):
+                    add(3, u, h)
+            out1(1, 2, False)
+            out1(1, 3, False)

@@ -18,8 +18,8 @@ ACT = mybir.ActivationFunctionType
 FLOPS = 3 * 2 * T * HID * 512
 BYTES = 2 * (B * C * H * W + HID * K1 + OC * HID + T * OC) + 4 * (T * HID + B * C * H * W + HID * K1)
 G = 4
-UNITS = ((0, 0), (0, 1), (1, 0), (0, 2), (1, 1), (0, 3), (1, 2), (1, 3))
-ZG = (0, 1)
+UNITS = ((0, 0), (0, 1), (0, 2), (1, 0), (0, 3), (1, 1), (1, 2), (1, 3))
+ZG = ()
 BUFS = {"dh": 4, "tr": 2, "acc": 2}
 NU = 8
 
@@ -68,7 +68,7 @@ def tile_memoryefficientpatchdownscale_v_kernel(
                 nc.gpsimd.memset(part.rearrange("p (s d w) -> p d s w", s=6, d=5)[:, z], 0)
 
         graw, wraw, xraw, o1t, rt, dzi, xsb = {}, {}, {}, {}, {}, {}, {}
-        mixed, hidi, dhb, trb, accb, stg = {}, {}, {}, {}, {}, {}
+        mixed, hidi, dhb, trb, accb, stg, dzn = {}, {}, {}, {}, {}, {}, {}
 
         def load_g(g):
             graw[g] = rot.tile([P, 4, 512], BF16, name="graw", tag="graw", bufs=4)
@@ -106,10 +106,20 @@ def tile_memoryefficientpatchdownscale_v_kernel(
 
         def mix_w2(f):
             d = mix_tile(("w2", f))
-            nc.scalar.mul(
-                out=d[:].rearrange("p (m t j) -> p m j t", t=4, j=4),
-                in_=wraw[2, f][:].rearrange("p j (m t) -> p m j t", t=4),
-                mul=-0.5,
+            view = d[:].rearrange("p (m t j) -> p m j t", t=4, j=4)
+            raw = wraw[2, f][:].rearrange("p j (m t) -> p m j t", t=4)
+            cut = 64 if f == 0 else 128
+            nc.scalar.mul(out=view[:, :cut], in_=raw[:, :cut], mul=-0.5)
+            if f == 0:
+                nc.vector.tensor_scalar(
+                    out=view[:, cut:], in0=raw[:, cut:], scalar1=-0.5, scalar2=None, op0=ALU.mult
+                )
+
+        def mix_w1(f):
+            d = mix_tile(("w1", f))
+            nc.scalar.copy(
+                out=d[:].rearrange("p (t m j) -> p m j t", t=4, j=4),
+                in_=wraw[1, f][:].rearrange("p j (m t) -> p m j t", t=4),
             )
 
         def move(raw, ident, h):
@@ -212,31 +222,31 @@ def tile_memoryefficientpatchdownscale_v_kernel(
                 )
 
         def d2(n):
-            dzi[n] = rot.tile([P, 2048], BF16, name="dzi", tag="dzi", bufs=2, align_bytes=64)
+            dzn[n] = rot.tile([P, 4, 512], BF16, name="dzn", tag="dzn", bufs=2)
             nc.vector.scalar_tensor_tensor(
-                out=dzi[n][:].rearrange("p (h j) -> p h j", j=4),
-                in0=o1t[n][:].rearrange("p j h -> p h j"),
-                scalar=1.0,
-                in1=rt[n][:].rearrange("p j h -> p h j"),
-                op0=ALU.add,
-                op1=ALU.mult,
+                out=dzn[n][:], in0=o1t[n][:], scalar=1.0, in1=rt[n][:], op0=ALU.add, op1=ALU.mult
+            )
+
+        def mix_dz(n):
+            dzi[n] = rot.tile([P, 2048], BF16, name="dzi", tag="dzi", bufs=1, align_bytes=64)
+            nc.vector.tensor_copy(
+                out=dzi[n][:].rearrange("p (m t j) -> p m j t", t=4, j=4),
+                in_=dzn[n][:].rearrange("p j (m t) -> p m j t", t=4),
             )
 
         def tr(n):
-            words = dzi[n][:].bitcast(F32)
-            for u in range(2):
+            for b in range(2):
                 bank = psum.tile([P, 4, P], F32, name="tr", tag="tr", bufs=2)
-                trb[n, u] = bank
-                for t in range(4):
-                    nc.tensor.transpose(bank[:, t, :], words[:, 2 * t + u : 1024 : 8], idf[:])
+                trb[n, b] = bank
+                for k in range(4):
+                    words = dzn[n][:, 2 * b + k // 2, :].bitcast(F32)
+                    nc.tensor.transpose(bank[:, k, :], words[:, k % 2 : 256 : 2], idf[:])
 
         def cp_tr(n):
             hidi[n] = rot.tile([P, 2048], BF16, name="hidi", tag="hidi", bufs=2, align_bytes=64)
-            for u in range(2):
-                nc.scalar.copy(
-                    out=hidi[n][:].rearrange("m (p u e t) -> m u p e t", u=2, e=2, t=4)[:, u],
-                    in_=trb[n, u][:].rearrange("m t p -> m (t p)").bitcast(BF16).rearrange("m (t p e) -> m p e t", t=4, e=2),
-                )
+            words = hidi[n][:].bitcast(F32).rearrange("m (p b k) -> m b p k", b=2, k=4)
+            for b in range(2):
+                nc.scalar.copy(out=words[:, b], in_=trb[n, b][:].rearrange("m k p -> m p k"))
 
         def sort_x(g):
             xsb[g] = rot.tile([P, 2, 4, P], F32, name="xs", tag="xs", bufs=1)
@@ -291,16 +301,16 @@ def tile_memoryefficientpatchdownscale_v_kernel(
             copy(out=stg[g, u][:, v, :], in_=accb[g, q][:])
 
         def add(g, u, h):
-            if (g, "o") not in accb:
-                accb[g, "o"] = rot.tile([P, 2048], F32, name="o0t", tag="o0t", bufs=2)
-            o = accb[g, "o"]
+            if u == 0:
+                accb[g, h, "o"] = rot.tile([P, 1024], F32, name="o0t", tag="o0t", bufs=3)
+            o = accb[g, h, "o"]
             if g in ZG:
                 src = accb[g, u, h][:].rearrange("c (v t) -> c v t", v=2)
             else:
                 src = stg[g, u][:, :, h * 256 : h * 256 + 256]
             pl = pooled[:, g * 512 + h * 256 : g * 512 + h * 256 + 256]
             nc.vector.scalar_tensor_tensor(
-                out=o[:, h * 1024 : h * 1024 + 1024].rearrange("c (i u j v) -> c u i j v", u=2, j=32, v=2)[:, u],
+                out=o[:].rearrange("c (i u j v) -> c u i j v", u=2, j=32, v=2)[:, u],
                 in0=pl.rearrange("c (i j) -> c i j", j=32).unsqueeze(3).to_broadcast([P, 8, 32, 2]),
                 scalar=0.25,
                 in1=src.rearrange("c v (i j) -> c i j v", j=32),
@@ -309,7 +319,7 @@ def tile_memoryefficientpatchdownscale_v_kernel(
             )
             if u == 1:
                 b, s = divmod(g, 2)
-                nc.sync.dma_start(out=o0v[b, s, :, h * 1024 : h * 1024 + 1024], in_=o[:, h * 1024 : h * 1024 + 1024])
+                nc.sync.dma_start(out=o0v[b, s, :, h * 1024 : h * 1024 + 1024], in_=o[:])
 
         def dw1(f, t, gs, tag):
             if gs[0] == 0:
@@ -328,136 +338,124 @@ def tile_memoryefficientpatchdownscale_v_kernel(
             nc.sync.dma_start(out=o1o[f, t], in_=res[:])
 
         with tc.manual_schedule():
-            load_w(2, 0)
             load_g(0)
+            load_w(2, 0)
             load_o1(0)
             load_g(1)
             load_o1(1)
+            load_g(2)
+            load_x(0)
             load_w(2, 1)
             load_o1(2)
-            load_x(0)
-            load_g(2)
-            load_w(1, 0)
-            load_o1(3)
+            load_g(3)
             load_x(1)
+            load_o1(3)
 
             nc.scalar.activation(out=warm[:], in_=warm[:], func=ACT.Silu, scale=-1.0)
-            mix_w2(0)
             mix_g(0)
+            mix_w2(0)
             q_g(0)
             q_w2(0)
             pool_mm(0)
             dh(0)
             silu(0)
-            mix_g(1)
             tanh(0)
             cp_pool(0)
 
             for n in range(NU):
-                f, g = UNITS[n]
                 last = n == NU - 1
-                if n > 0:
-                    cp_tr(n - 1)
-                if n in (4, 6):
-                    dp(n // 2 - 2, 0, 0)
-                    dp(n // 2 - 2, 1, 0)
-                if last:
-                    for t in (2, 3):
-                        dw1(0, t, range(G), "acc")
-                        out1(0, t, False)
                 d1(n)
                 if n == 0:
-                    q_g(1)
-                if n == 1:
-                    q_w2(1)
+                    mix_g(1)
+                if n > 0:
+                    q_hid(n - 1)
+                if n in (0, 1):
+                    if n == 1:
+                        q_g(2)
                 if n == 2:
-                    q_g(2)
+                    q_w2(1)
                 if n == 3:
+                    q_g(3)
+                if n == 4:
                     q_w1(0)
                     q_w1(1)
-                if n == 4:
-                    q_g(3)
+                if n == 0:
+                    d2(n)
+                    q_g(1)
+                if 1 <= n <= 4:
+                    tr_x(n - 1)
                 if not last:
                     dh(n + 1)
                     silu(n + 1)
                 else:
-                    q_hid(n - 1)
-                    for q in range(2):
-                        dps(2, q)
-                        stage(2, q)
-                    for t in range(2):
-                        dw1(1, t, range(3), "dh")
-                if n in (4, 6):
-                    gz = n // 2 - 2
-                    add(gz, 0, 0)
-                    add(gz, 1, 0)
-                    dp(gz, 0, 1)
-                    dp(gz, 1, 1)
-                if 2 <= n <= 5:
-                    tr_x(n - 2)
-                    cp_x(n - 2)
-                d2(n)
+                    dw1(1, 0, range(3), "dh")
+                    dw1(1, 1, range(3), "dh")
+                if 5 <= n:
+                    for q in range(4):
+                        dps(n - 5, q)
+                        stage(n - 5, q)
+                if 1 <= n <= 4:
+                    cp_x(n - 1)
+                if n > 0:
+                    d2(n)
                 if not last:
                     tanh(n + 1)
                 tr(n)
+                cp_tr(n)
                 if n + 4 < NU:
                     load_o1(n + 4)
                 if n == 0:
-                    load_g(3)
+                    load_w(1, 0)
+                if n == 1:
                     load_w(1, 1)
                 if n in (1, 2):
                     load_x(n + 1)
-                if n in (0, 2, 4):
-                    gg = n // 2 + 1
-                    pool_mm(gg)
-                    cp_pool(gg)
+                if n < G:
+                    sort_x(n)
+                mix_dz(n)
+                if n == 0:
+                    mix_g(2)
+                if 1 <= n <= G:
+                    q_p(n - 1)
+                if 5 <= n:
+                    add(n - 5, 0, 0)
+                    add(n - 5, 0, 1)
+                q_tok(n)
+                if 5 <= n and not last:
+                    add(n - 5, 1, 0)
+                    add(n - 5, 1, 1)
+                if n + 1 < G:
+                    pool_mm(n + 1)
+                    cp_pool(n + 1)
                 if n == 0:
                     pe_mix_w2(1)
                 if n == 1:
-                    mix_g(2)
-                    pe_mix(wraw[1, 0], ("w1", 0))
-                if n == 2:
-                    pe_mix(wraw[1, 1], ("w1", 1))
-                if n == 3:
                     pe_mix(graw[3], ("g", 3))
-                if 0 < n and not last:
-                    q_hid(n - 1)
-                if 1 <= n <= G:
-                    sort_x(n - 1)
-                if last:
-                    for q in (2, 3):
-                        dps(2, q)
-                        stage(2, q)
-                    cp_tr(n)
-                q_tok(n)
-                if 2 <= n <= 5:
-                    q_p(n - 2)
-                if n in (4, 6):
-                    add(gz, 0, 1)
-                    add(gz, 1, 1)
-                if n == 6:
-                    for t in (0, 1):
+                if n in (2, 3):
+                    pe_mix(wraw[1, n - 2], ("w1", n - 2))
+                if n in (4, 5):
+                    for t in (2 * n - 8, 2 * n - 7):
                         dw1(0, t, range(G), "acc")
                         out1(0, t, False)
-            add(2, 0, 0)
-            add(2, 1, 0)
-            q_hid(NU - 1)
-            add(2, 0, 1)
-            add(2, 1, 1)
-            for t in range(2):
+            for t in (0, 1):
                 dw1(1, t, [3], "dh")
+            dw1(1, 2, range(G), "dh")
+            q_hid(NU - 1)
+            add(2, 1, 0)
+            add(2, 1, 1)
+            out1(1, 0, False)
+            out1(1, 1, True)
             dps(3, 0)
             dps(3, 1)
             dps(3, 2, "tr")
             dps(3, 3, "tr")
-            out1(1, 0, False)
-            out1(1, 1, True)
-            for q in range(4):
-                stage(3, q, q % 2 == 1)
-            for t in (2, 3):
-                dw1(1, t, range(G), "dh")
-            for h in range(2):
-                for u in range(2):
+            dw1(1, 3, range(G), "dh")
+            stage(3, 0)
+            stage(3, 1, True)
+            stage(3, 2)
+            stage(3, 3)
+            for u in range(2):
+                for h in range(2):
                     add(3, u, h)
             out1(1, 2, False)
             out1(1, 3, False)

@@ -18,8 +18,8 @@ ACT = mybir.ActivationFunctionType
 FLOPS = 3 * 2 * T * HID * 512
 BYTES = 2 * (B * C * H * W + HID * K1 + OC * HID + T * OC) + 4 * (T * HID + B * C * H * W + HID * K1)
 G = 4
+CUT = (64, 64)
 UNITS = ((0, 0), (0, 1), (0, 2), (1, 0), (0, 3), (1, 1), (1, 2), (1, 3))
-ZG = ()
 BUFS = {"dh": 4, "tr": 2, "acc": 2}
 NU = 8
 
@@ -44,7 +44,6 @@ def tile_memoryefficientpatchdownscale_v_kernel(
         warm = keep.tile([P, 1], F32, name="warm")
         idf = keep.tile([P, P], F32, name="idf")
         idb = keep.tile([P, P], BF16, name="idb")
-        idn = keep.tile([P, P], BF16, name="idn")
         g_c = keep.tile([P, T], U32, name="g_c", align_bytes=64)
         g_s = keep.tile([P, T], U8, name="g_s", align_bytes=64)
         w2_c = keep.tile([P, HID], U32, name="w2_c", align_bytes=64)
@@ -55,17 +54,13 @@ def tile_memoryefficientpatchdownscale_v_kernel(
         p_s = keep.tile([P, G * 512], U8, name="p_s", align_bytes=64)
         tok_c = keep.tile([P, G * HID], U32, name="tok_c", align_bytes=64)
         tok_s = keep.tile([P, G * HID], U8, name="tok_s", align_bytes=64)
-        hid_c = keep.tile([P, 6 * 1280], U32, name="hid_c", align_bytes=64)
-        hid_s = keep.tile([P, 6 * 1280], U8, name="hid_s", align_bytes=64)
+        hid_c = keep.tile([P, 2 * T], U32, name="hid_c", align_bytes=64)
+        hid_s = keep.tile([P, 2 * T], U8, name="hid_s", align_bytes=64)
         pooled = keep.tile([P, T], F32, name="pooled")
 
         nc.vector.memset(warm[:], 0.0)
         make_identity(nc, idf[:])
         make_identity(nc, idb[:])
-        nc.vector.tensor_scalar(out=idn[:], in0=idb[:], scalar1=-0.5, scalar2=None, op0=ALU.mult)
-        for part in (hid_c[:], hid_s[:].bitcast(U32)):
-            for z in (0, 2, 4):
-                nc.gpsimd.memset(part.rearrange("p (s d w) -> p d s w", s=6, d=5)[:, z], 0)
 
         graw, wraw, xraw, o1t, rt, dzi, xsb = {}, {}, {}, {}, {}, {}, {}
         mixed, hidi, dhb, trb, accb, stg, dzn = {}, {}, {}, {}, {}, {}, {}
@@ -85,16 +80,17 @@ def tile_memoryefficientpatchdownscale_v_kernel(
             b, s = divmod(g, 2)
             nc.sync.dma_start(out=xraw[g][:], in_=xv[b, s])
 
-        def load_o1(n):
+        def load_o1(n, js=(0, 2)):
             f, g = UNITS[n]
-            o1t[n] = rot.tile([P, 4, 512], F32, name="o1t", tag="o1t", bufs=4)
-            for j in (0, 2):
+            if 0 in js:
+                o1t[n] = rot.tile([P, 4, 512], F32, name="o1t", tag="o1t", bufs=4)
+            for j in js:
                 nc.sync.dma_start(
                     out=o1t[n][:, j : j + 2, :], in_=o1v[g, :, j : j + 2, f * 512 : (f + 1) * 512]
                 )
 
         def mix_tile(key):
-            mixed[key] = rot.tile([P, 2048], BF16, name="mix", tag="mix", bufs=2, align_bytes=64)
+            mixed[key] = rot.tile([P, 2048], BF16, name="mix", tag="mix", bufs=3, align_bytes=64)
             return mixed[key]
 
         def mix_g(g):
@@ -108,9 +104,10 @@ def tile_memoryefficientpatchdownscale_v_kernel(
             d = mix_tile(("w2", f))
             view = d[:].rearrange("p (m t j) -> p m j t", t=4, j=4)
             raw = wraw[2, f][:].rearrange("p j (m t) -> p m j t", t=4)
-            cut = 64 if f == 0 else 128
-            nc.scalar.mul(out=view[:, :cut], in_=raw[:, :cut], mul=-0.5)
-            if f == 0:
+            cut = CUT[f]
+            if cut:
+                nc.scalar.mul(out=view[:, :cut], in_=raw[:, :cut], mul=-0.5)
+            if cut < 128:
                 nc.vector.tensor_scalar(
                     out=view[:, cut:], in0=raw[:, cut:], scalar1=-0.5, scalar2=None, op0=ALU.mult
                 )
@@ -121,32 +118,6 @@ def tile_memoryefficientpatchdownscale_v_kernel(
                 out=d[:].rearrange("p (t m j) -> p m j t", t=4, j=4),
                 in_=wraw[1, f][:].rearrange("p j (m t) -> p m j t", t=4),
             )
-
-        def move(raw, ident, h):
-            bank = psum.tile([P, 4, 256], BF16, name="acc", tag="acc", bufs=BUFS["acc"])
-            for j in range(4):
-                nc.tensor.matmul(
-                    bank[:, j, :], lhsT=ident[:], rhs=raw[:, j, h * 256 : h * 256 + 256], start=True, stop=True
-                )
-            return bank
-
-        def pe_mix_w2(f):
-            d = mix_tile(("w2", f))
-            for h in range(2):
-                bank = move(wraw[2, f], idn, h)
-                nc.scalar.copy(
-                    out=d[:, h * 1024 : h * 1024 + 1024].rearrange("p (c j) -> p c j", j=4),
-                    in_=bank[:].rearrange("p j c -> p c j"),
-                )
-
-        def pe_mix(raw, key):
-            d = mix_tile(key)
-            for h in range(2):
-                bank = move(raw, idb, h)
-                nc.scalar.copy(
-                    out=d[:].rearrange("p (t m j) -> p t m j", t=4, j=4)[:, :, h * 64 : h * 64 + 64, :],
-                    in_=bank[:].rearrange("p j (m t) -> p t m j", t=4),
-                )
 
         def quant(src, codes, scales, c0, fmt):
             nc.vector.quantize_mx(
@@ -169,16 +140,9 @@ def tile_memoryefficientpatchdownscale_v_kernel(
             f, g = UNITS[n]
             quant(dzi[n], tok_c, tok_s, g * HID + f * 512, E5)
 
-        def slot(f, g):
-            return 1280 * (g if f == 0 else 4 + g % 2)
-
         def q_hid(n):
             f, g = UNITS[n]
-            c0 = slot(f, g) + 256
-            cuts = ((0, 1024, 0), (1024, 2048, 512)) if g in ZG else ((0, 2048, 0),)
-            for a, b, d in cuts:
-                c = slice(c0 + d, c0 + d + (b - a) // 4)
-                nc.vector.quantize_mx(out=hid_c[:, c].bitcast(E5), scales=hid_s[:, c], in_=hidi[n][:, a:b])
+            quant(hidi[n], hid_c, hid_s, f * T + g * 512, E5)
 
         def mx(out, lc, ls, l0, lf, rc, rs, r0, rf, start, stop):
             nc.tensor.matmul_mx(
@@ -228,7 +192,7 @@ def tile_memoryefficientpatchdownscale_v_kernel(
             )
 
         def mix_dz(n):
-            dzi[n] = rot.tile([P, 2048], BF16, name="dzi", tag="dzi", bufs=1, align_bytes=64)
+            dzi[n] = rot.tile([P, 2048], BF16, name="dzi", tag="dzi", bufs=2, align_bytes=64)
             nc.vector.tensor_copy(
                 out=dzi[n][:].rearrange("p (m t j) -> p m j t", t=4, j=4),
                 in_=dzn[n][:].rearrange("p j (m t) -> p m j t", t=4),
@@ -258,7 +222,7 @@ def tile_memoryefficientpatchdownscale_v_kernel(
 
         def tr_x(g):
             for u in range(2):
-                bank = psum.tile([P, 4, P], F32, name="tr", tag="tr", bufs=2)
+                bank = psum.tile([P, 4, P], F32, name="acc", tag="acc", bufs=2)
                 trb["x", g, u] = bank
                 for t in range(4):
                     nc.tensor.transpose(bank[:, t, :], xsb[g][:, u, t, :], idf[:])
@@ -281,22 +245,15 @@ def tile_memoryefficientpatchdownscale_v_kernel(
         def cp_pool(g):
             nc.scalar.copy(out=pooled[:, g * 512 : (g + 1) * 512], in_=accb["p", g][:])
 
-        def dp(g, u, h, tag="acc"):
-            accb[g, u, h] = psum.tile([P, 512], F32, name=tag, tag=tag, bufs=BUFS[tag])
-            for f in range(2):
-                for v in range(2):
-                    c0 = slot(f, g) + 512 * h + 256 * (1 - v)
-                    mx(accb[g, u, h], w1_c, w1_s, f * 512 + (2 * u + v) * 128, E4, hid_c, hid_s, c0, E5, f + v == 0, f + v == 2)
-
         def dps(g, q, tag="acc"):
             accb[g, q] = psum.tile([P, 512], F32, name=tag, tag=tag, bufs=BUFS[tag])
             for f in range(2):
-                mx(accb[g, q], w1_c, w1_s, f * 512 + q * 128, E4, hid_c, hid_s, slot(f, g) + 256, E5, f == 0, f == 1)
+                mx(accb[g, q], w1_c, w1_s, f * 512 + q * 128, E4, hid_c, hid_s, f * T + g * 512, E5, f == 0, f == 1)
 
         def stage(g, q, on_vector=False):
             u, v = divmod(q, 2)
             if v == 0:
-                stg[g, u] = rot.tile([P, 2, 512], F32, name="stg", tag="stg", bufs=2)
+                stg[g, u] = rot.tile([P, 2, 512], F32, name="stg", tag="stg", bufs=3)
             copy = nc.vector.tensor_copy if on_vector else nc.scalar.copy
             copy(out=stg[g, u][:, v, :], in_=accb[g, q][:])
 
@@ -304,10 +261,7 @@ def tile_memoryefficientpatchdownscale_v_kernel(
             if u == 0:
                 accb[g, h, "o"] = rot.tile([P, 1024], F32, name="o0t", tag="o0t", bufs=3)
             o = accb[g, h, "o"]
-            if g in ZG:
-                src = accb[g, u, h][:].rearrange("c (v t) -> c v t", v=2)
-            else:
-                src = stg[g, u][:, :, h * 256 : h * 256 + 256]
+            src = stg[g, u][:, :, h * 256 : h * 256 + 256]
             pl = pooled[:, g * 512 + h * 256 : g * 512 + h * 256 + 256]
             nc.vector.scalar_tensor_tensor(
                 out=o[:].rearrange("c (i u j v) -> c u i j v", u=2, j=32, v=2)[:, u],
@@ -328,7 +282,7 @@ def tile_memoryefficientpatchdownscale_v_kernel(
                 mx(accb["w", f, t], tok_c, tok_s, g * HID + f * 512 + t * 128, E5, p_c, p_s, g * 512, E4, g == 0, g == 3)
 
         def out1(f, t, on_vector):
-            res = rot.tile([P, 512], F32, name="res", tag="res", bufs=3)
+            res = rot.tile([P, 512], F32, name="res", tag="res", bufs=4)
             dst = res[:].rearrange("m (c u v) -> m c u v", u=2, v=2)
             src = accb["w", f, t][:].rearrange("m (u c v) -> m c u v", u=2, v=2)
             if on_vector:
@@ -364,44 +318,46 @@ def tile_memoryefficientpatchdownscale_v_kernel(
 
             for n in range(NU):
                 last = n == NU - 1
+                if 1 <= n <= G:
+                    tr_x(n - 1)
+                    cp_x(n - 1)
                 d1(n)
                 if n == 0:
                     mix_g(1)
-                if n > 0:
+                if n >= 6:
                     q_hid(n - 1)
-                if n in (0, 1):
-                    if n == 1:
-                        q_g(2)
+                if n == 1:
+                    q_g(2)
                 if n == 2:
                     q_w2(1)
                 if n == 3:
                     q_g(3)
                 if n == 4:
                     q_w1(0)
+                if n == 5:
                     q_w1(1)
-                if n == 0:
-                    d2(n)
-                    q_g(1)
-                if 1 <= n <= 4:
-                    tr_x(n - 1)
-                if not last:
+                if not last and n > 0:
                     dh(n + 1)
                     silu(n + 1)
-                else:
-                    dw1(1, 0, range(3), "dh")
-                    dw1(1, 1, range(3), "dh")
+                if last:
+                    dw1(1, 0, range(2), "dh")
+                    dw1(1, 1, range(2), "dh")
                 if 5 <= n:
                     for q in range(4):
                         dps(n - 5, q)
                         stage(n - 5, q)
-                if 1 <= n <= 4:
-                    cp_x(n - 1)
-                if n > 0:
-                    d2(n)
+                d2(n)
+                if n == 0:
+                    q_g(1)
+                    dh(1)
+                    silu(1)
                 if not last:
                     tanh(n + 1)
                 tr(n)
                 cp_tr(n)
+                if n > 0:
+                    q_tok(n - 1)
+                mix_dz(n)
                 if n + 4 < NU:
                     load_o1(n + 4)
                 if n == 0:
@@ -410,52 +366,57 @@ def tile_memoryefficientpatchdownscale_v_kernel(
                     load_w(1, 1)
                 if n in (1, 2):
                     load_x(n + 1)
-                if n < G:
-                    sort_x(n)
-                mix_dz(n)
-                if n == 0:
-                    mix_g(2)
+                if 1 <= n <= 5:
+                    q_hid(n - 1)
                 if 1 <= n <= G:
                     q_p(n - 1)
+                if n == 0:
+                    mix_g(2)
+                if n == 1:
+                    mix_g(3)
+                if n < G:
+                    sort_x(n)
                 if 5 <= n:
                     add(n - 5, 0, 0)
-                    add(n - 5, 0, 1)
-                q_tok(n)
-                if 5 <= n and not last:
+                if last:
+                    q_tok(n)
+                    q_hid(n)
+                if 5 <= n:
                     add(n - 5, 1, 0)
+                if 5 <= n and not last:
+                    add(n - 5, 0, 1)
                     add(n - 5, 1, 1)
                 if n + 1 < G:
                     pool_mm(n + 1)
                     cp_pool(n + 1)
                 if n == 0:
-                    pe_mix_w2(1)
-                if n == 1:
-                    pe_mix(graw[3], ("g", 3))
+                    mix_w2(1)
                 if n in (2, 3):
-                    pe_mix(wraw[1, n - 2], ("w1", n - 2))
-                if n in (4, 5):
-                    for t in (2 * n - 8, 2 * n - 7):
+                    mix_w1(n - 2)
+                if n in (5, 6):
+                    for t in (2 * n - 10, 2 * n - 9):
                         dw1(0, t, range(G), "acc")
                         out1(0, t, False)
+            for t in (2, 3):
+                dw1(1, t, (0, 1), "dh")
             for t in (0, 1):
-                dw1(1, t, [3], "dh")
-            dw1(1, 2, range(G), "dh")
-            q_hid(NU - 1)
-            add(2, 1, 0)
-            add(2, 1, 1)
-            out1(1, 0, False)
-            out1(1, 1, True)
+                dw1(1, t, (2, 3), "dh")
             dps(3, 0)
             dps(3, 1)
             dps(3, 2, "tr")
             dps(3, 3, "tr")
-            dw1(1, 3, range(G), "dh")
+            for t in (2, 3):
+                dw1(1, t, (2, 3), "dh")
+            add(2, 0, 1)
+            add(2, 1, 1)
+            out1(1, 0, False)
+            out1(1, 1, True)
             stage(3, 0)
             stage(3, 1, True)
             stage(3, 2)
             stage(3, 3)
-            for u in range(2):
-                for h in range(2):
+            for h in range(2):
+                for u in range(2):
                     add(3, u, h)
             out1(1, 2, False)
             out1(1, 3, False)

@@ -3,38 +3,49 @@ from contextlib import ExitStack
 import concourse.mybir as mybir
 from concourse.masks import make_identity
 
-B, C, H, W = 2, 128, 64, 64
-HID, OC, K1 = 1024, 512, 512
-T = 2048
+BATCH, CHANNELS, SIDE = 2, 128, 64
+HIDDEN, OUT_CHANNELS, PATCH = 1024, 512, 512
+TOKENS = 2048
 P = 128
+PASS = 512
+GROUPS = TOKENS // PASS
+
 F32 = mybir.dt.float32
 BF16 = mybir.dt.bfloat16
 U32 = mybir.dt.uint32
 U8 = mybir.dt.uint8
-E4 = mybir.dt.float8_e4m3fn_x4
-E5 = mybir.dt.float8_e5m2_x4
+E4M3 = mybir.dt.float8_e4m3fn_x4
+E5M2 = mybir.dt.float8_e5m2_x4
 ALU = mybir.AluOpType
 ACT = mybir.ActivationFunctionType
-FLOPS = 3 * 2 * T * HID * 512
-BYTES = 2 * (B * C * H * W + HID * K1 + OC * HID + T * OC) + 4 * (T * HID + B * C * H * W + HID * K1)
-G = 4
-CUT = (64, 64)
+
+FLOPS = 2 * TOKENS * HIDDEN * (OUT_CHANNELS + PATCH + PATCH)
+BYTES = 2 * (BATCH * CHANNELS * SIDE * SIDE + HIDDEN * PATCH + OUT_CHANNELS * HIDDEN + TOKENS * OUT_CHANNELS) + 4 * (
+    TOKENS * HIDDEN + BATCH * CHANNELS * SIDE * SIDE + HIDDEN * PATCH
+)
+
 UNITS = ((0, 0), (0, 1), (0, 2), (1, 0), (0, 3), (1, 1), (1, 2), (1, 3))
-BUFS = {"dh": 4, "tr": 2, "acc": 2}
-NU = 8
+LAST = len(UNITS) - 1
+
+BANKS = {"dh": 4, "tr": 2, "acc": 2}
+
+W2_ON_SCALAR = (64, 128)
+
+GPSIMD_COLUMNS = 384
 
 
 def tile_memoryefficientpatchdownscale_v_kernel(
     tc, x, weight1, bias1, weight2, bias2, o1, grad_out, out_0, out_1
 ):
     nc = tc.nc
-    go = grad_out.rearrange("b (p j) y w -> b p j (y w)", j=4)
-    w2v = weight2.rearrange("(p j) h -> p j h", j=4)
-    w1v = weight1.rearrange("(f p j) k -> f p j k", p=P, j=4)
-    o1v = o1.rearrange("(g p j) h -> g p j h", p=P, j=4)
-    xv = x.rearrange("b c (s r) w -> b s c (r w)", s=2)
-    o0v = out_0.rearrange("b c (s r) w -> b s c (r w)", s=2)
-    o1o = out_1.rearrange("(f t m) k -> f t m k", m=P, t=4)
+
+    g_hbm = grad_out.rearrange("b (p s) y w -> b p s (y w)", s=4)
+    w2_hbm = weight2.rearrange("(p s) h -> p s h", s=4)
+    w1_hbm = weight1.rearrange("(f p s) k -> f p s k", p=P, s=4)
+    o1_hbm = o1.rearrange("(g p s) h -> g p s h", p=P, s=4)
+    x_hbm = x.rearrange("b c (part r) w -> b part c (r w)", part=2)
+    out_0_hbm = out_0.rearrange("b c (part r) w -> b part c (r w)", part=2)
+    out_1_hbm = out_1.rearrange("(f block m) k -> f block m k", m=P, block=4)
 
     with ExitStack() as ctx:
         keep = ctx.enter_context(tc.tile_pool(name="keep", bufs=1))
@@ -42,266 +53,303 @@ def tile_memoryefficientpatchdownscale_v_kernel(
         psum = ctx.enter_context(tc.psum_pool(name="psum", bufs=2))
 
         warm = keep.tile([P, 1], F32, name="warm")
-        idf = keep.tile([P, P], F32, name="idf")
-        idb = keep.tile([P, P], BF16, name="idb")
-        g_c = keep.tile([P, T], U32, name="g_c", align_bytes=64)
-        g_s = keep.tile([P, T], U8, name="g_s", align_bytes=64)
-        w2_c = keep.tile([P, HID], U32, name="w2_c", align_bytes=64)
-        w2_s = keep.tile([P, HID], U8, name="w2_s", align_bytes=64)
-        w1_c = keep.tile([P, 2 * K1], U32, name="w1_c", align_bytes=64)
-        w1_s = keep.tile([P, 2 * K1], U8, name="w1_s", align_bytes=64)
-        p_c = keep.tile([P, G * 512], U32, name="p_c", align_bytes=64)
-        p_s = keep.tile([P, G * 512], U8, name="p_s", align_bytes=64)
-        tok_c = keep.tile([P, G * HID], U32, name="tok_c", align_bytes=64)
-        tok_s = keep.tile([P, G * HID], U8, name="tok_s", align_bytes=64)
-        hid_c = keep.tile([P, 2 * T], U32, name="hid_c", align_bytes=64)
-        hid_s = keep.tile([P, 2 * T], U8, name="hid_s", align_bytes=64)
-        pooled = keep.tile([P, T], F32, name="pooled")
+        ident_f32 = keep.tile([P, P], F32, name="ident_f32")
+        ident_bf16 = keep.tile([P, P], BF16, name="ident_bf16")
+        pooled = keep.tile([P, TOKENS], F32, name="pooled")
+
+        def mx_tiles(columns, name):
+            codes = keep.tile([P, columns], U32, name=name + "_codes", align_bytes=64)
+            scales = keep.tile([P, columns], U8, name=name + "_scales", align_bytes=64)
+            return codes, scales
+
+        g_mx = mx_tiles(TOKENS, "g")
+        w2_mx = mx_tiles(HIDDEN, "w2")
+        w1_mx = mx_tiles(2 * PATCH, "w1")
+        p_mx = mx_tiles(GROUPS * PATCH, "p")
+        tok_mx = mx_tiles(GROUPS * HIDDEN, "tok")
+        hid_mx = mx_tiles(2 * TOKENS, "hid")
 
         nc.vector.memset(warm[:], 0.0)
-        make_identity(nc, idf[:])
-        make_identity(nc, idb[:])
+        make_identity(nc, ident_f32[:])
+        make_identity(nc, ident_bf16[:])
 
-        graw, wraw, xraw, o1t, rt, dzi, xsb = {}, {}, {}, {}, {}, {}, {}
-        mixed, hidi, dhb, trb, accb, stg, dzn = {}, {}, {}, {}, {}, {}, {}
+        g_raw, w_raw, x_raw, x_sorted = {}, {}, {}, {}
+        mixed = {}
+        tanh_o1, factor, dz = {}, {}, {}
+        bank = {}
+        staged, pixels = {}, {}
 
         def load_g(g):
-            graw[g] = rot.tile([P, 4, 512], BF16, name="graw", tag="graw", bufs=4)
-            b, s = divmod(g, 2)
-            nc.sync.dma_start(out=graw[g][:], in_=go[b, :, :, s * 512 : (s + 1) * 512])
+            g_raw[g] = rot.tile([P, 4, 512], BF16, name="g_raw", tag="g_raw", bufs=4)
+            image, part = divmod(g, 2)
+            nc.sync.dma_start(out=g_raw[g][:], in_=g_hbm[image, :, :, part * 512 : (part + 1) * 512])
 
-        def load_w(which, f):
-            wraw[which, f] = rot.tile([P, 4, 512], BF16, name="wraw", tag="wraw", bufs=3)
-            src = w2v[:, :, f * 512 : (f + 1) * 512] if which == 2 else w1v[f]
-            nc.sync.dma_start(out=wraw[which, f][:], in_=src)
+        def load_w2(f):
+            w_raw["w2", f] = rot.tile([P, 4, 512], BF16, name="w_raw", tag="w_raw", bufs=3)
+            nc.sync.dma_start(out=w_raw["w2", f][:], in_=w2_hbm[:, :, f * 512 : (f + 1) * 512])
+
+        def load_w1(f):
+            w_raw["w1", f] = rot.tile([P, 4, 512], BF16, name="w_raw", tag="w_raw", bufs=3)
+            nc.sync.dma_start(out=w_raw["w1", f][:], in_=w1_hbm[f])
 
         def load_x(g):
-            xraw[g] = rot.tile([P, 2048], BF16, name="xraw", tag="xraw", bufs=2)
-            b, s = divmod(g, 2)
-            nc.sync.dma_start(out=xraw[g][:], in_=xv[b, s])
+            x_raw[g] = rot.tile([P, 2048], BF16, name="x_raw", tag="x_raw", bufs=2)
+            image, part = divmod(g, 2)
+            nc.sync.dma_start(out=x_raw[g][:], in_=x_hbm[image, part])
 
-        def load_o1(n, js=(0, 2)):
+        def load_o1(n):
             f, g = UNITS[n]
-            if 0 in js:
-                o1t[n] = rot.tile([P, 4, 512], F32, name="o1t", tag="o1t", bufs=4)
-            for j in js:
+            tanh_o1[n] = rot.tile([P, 4, 512], F32, name="o1t", tag="o1t", bufs=4)
+            for s in (0, 2):
                 nc.sync.dma_start(
-                    out=o1t[n][:, j : j + 2, :], in_=o1v[g, :, j : j + 2, f * 512 : (f + 1) * 512]
+                    out=tanh_o1[n][:, s : s + 2, :], in_=o1_hbm[g, :, s : s + 2, f * 512 : (f + 1) * 512]
                 )
 
-        def mix_tile(key):
+        def new_mix(key):
             mixed[key] = rot.tile([P, 2048], BF16, name="mix", tag="mix", bufs=3, align_bytes=64)
             return mixed[key]
 
-        def mix_g(g):
-            d = mix_tile(("g", g))
-            nc.vector.tensor_copy(
-                out=d[:].rearrange("p (t m j) -> p m j t", t=4, j=4),
-                in_=graw[g][:].rearrange("p j (m t) -> p m j t", t=4),
-            )
+        def new_gpsimd_mix(key):
+            mixed[key] = rot.tile([P, 2048], BF16, name="mix_gp", tag="mix_gp", bufs=1, align_bytes=64)
+            return mixed[key]
 
-        def mix_w2(f):
-            d = mix_tile(("w2", f))
-            view = d[:].rearrange("p (m t j) -> p m j t", t=4, j=4)
-            raw = wraw[2, f][:].rearrange("p j (m t) -> p m j t", t=4)
-            cut = CUT[f]
-            if cut:
-                nc.scalar.mul(out=view[:, :cut], in_=raw[:, :cut], mul=-0.5)
-            if cut < 128:
-                nc.vector.tensor_scalar(
-                    out=view[:, cut:], in0=raw[:, cut:], scalar1=-0.5, scalar2=None, op0=ALU.mult
-                )
+        def natural(tile):
+            return tile.rearrange("p (m t s) -> p m s t", t=4, s=4)
+
+        def permuted(tile):
+            return tile.rearrange("p (t m s) -> p m s t", t=4, s=4)
+
+        def by_slot(tile):
+            return tile.rearrange("p s (m t) -> p m s t", t=4)
+
+        def mix_g(g):
+            nc.vector.tensor_copy(out=permuted(new_mix(("g", g))[:]), in_=by_slot(g_raw[g][:]))
 
         def mix_w1(f):
-            d = mix_tile(("w1", f))
-            nc.scalar.copy(
-                out=d[:].rearrange("p (t m j) -> p m j t", t=4, j=4),
-                in_=wraw[1, f][:].rearrange("p j (m t) -> p m j t", t=4),
+            nc.vector.tensor_copy(out=permuted(new_mix(("w1", f))[:]), in_=by_slot(w_raw["w1", f][:]))
+
+        def mix_w2(f):
+            dst, src = natural(new_mix(("w2", f))[:]), by_slot(w_raw["w2", f][:])
+            cut = W2_ON_SCALAR[f]
+            nc.scalar.mul(out=dst[:, :cut], in_=src[:, :cut], mul=-0.5)
+            if cut < 128:
+                nc.vector.tensor_scalar(out=dst[:, cut:], in0=src[:, cut:], scalar1=-0.5, scalar2=None, op0=ALU.mult)
+
+        def gpsimd_copy(out, in_):
+            nc.gpsimd.tensor_scalar(out=out, in0=in_, scalar1=1.0, scalar2=0.0, op0=ALU.mult, op1=ALU.add)
+
+        def gpsimd_mix_g(g):
+            quads = GPSIMD_COLUMNS // 4
+            gpsimd_copy(
+                new_gpsimd_mix(("g", g))[:].rearrange("p (t m s) -> p t m s", t=4, s=4)[:, :, :quads, :],
+                g_raw[g][:].rearrange("p s (m t) -> p t m s", t=4)[:, :, :quads, :],
             )
 
-        def quant(src, codes, scales, c0, fmt):
-            nc.vector.quantize_mx(
-                out=codes[:, c0 : c0 + 512].bitcast(fmt), scales=scales[:, c0 : c0 + 512], in_=src[:]
+        def rest_mix_g(g):
+            quads = GPSIMD_COLUMNS // 4
+            nc.vector.tensor_copy(out=permuted(mixed["g", g][:])[:, quads:], in_=by_slot(g_raw[g][:])[:, quads:])
+
+        def mix_dz(n):
+            nc.vector.tensor_copy(out=natural(new_gpsimd_mix(("tok", n))[:]), in_=by_slot(dz[n][:]))
+
+        def gpsimd_mix_dz(n):
+            gpsimd_copy(
+                new_gpsimd_mix(("tok", n))[:, : 4 * GPSIMD_COLUMNS].rearrange("p (h s) -> p h s", s=4),
+                dz[n][:, :, :GPSIMD_COLUMNS].rearrange("p s h -> p h s"),
             )
+
+        def rest_mix_dz(n):
+            nc.vector.tensor_copy(
+                out=natural(mixed["tok", n][:, 4 * GPSIMD_COLUMNS :]), in_=by_slot(dz[n][:, :, GPSIMD_COLUMNS:])
+            )
+
+        def quantize(key, mx, column, fmt):
+            codes, scales = mx
+            cols = slice(column, column + 512)
+            nc.vector.quantize_mx(out=codes[:, cols].bitcast(fmt), scales=scales[:, cols], in_=mixed[key][:])
 
         def q_g(g):
-            quant(mixed["g", g], g_c, g_s, g * 512, E5)
+            quantize(("g", g), g_mx, g * 512, E5M2)
 
         def q_w2(f):
-            quant(mixed["w2", f], w2_c, w2_s, f * 512, E4)
+            quantize(("w2", f), w2_mx, f * 512, E4M3)
 
         def q_w1(f):
-            quant(mixed["w1", f], w1_c, w1_s, f * 512, E4)
+            quantize(("w1", f), w1_mx, f * PATCH, E4M3)
 
         def q_p(g):
-            quant(mixed["p", g], p_c, p_s, g * 512, E4)
+            quantize(("p", g), p_mx, g * PATCH, E4M3)
 
         def q_tok(n):
             f, g = UNITS[n]
-            quant(dzi[n], tok_c, tok_s, g * HID + f * 512, E5)
+            quantize(("tok", n), tok_mx, g * HIDDEN + f * 512, E5M2)
 
         def q_hid(n):
             f, g = UNITS[n]
-            quant(hidi[n], hid_c, hid_s, f * T + g * 512, E5)
+            quantize(("hid", n), hid_mx, f * TOKENS + g * 512, E5M2)
 
-        def mx(out, lc, ls, l0, lf, rc, rs, r0, rf, start, stop):
+        def mx_pass(out, stationary, column, stationary_fmt, moving, moving_column, moving_fmt, start, stop):
+            cols = slice(column, column + P)
+            moving_cols = slice(moving_column, moving_column + PASS)
             nc.tensor.matmul_mx(
                 out=out[:],
-                lhsT=lc[:, l0 : l0 + 128].bitcast(lf),
-                lhsT_scale=ls[:, l0 : l0 + 128],
-                rhs=rc[:, r0 : r0 + 512].bitcast(rf),
-                rhs_scale=rs[:, r0 : r0 + 512],
+                lhsT=stationary[0][:, cols].bitcast(stationary_fmt),
+                lhsT_scale=stationary[1][:, cols],
+                rhs=moving[0][:, moving_cols].bitcast(moving_fmt),
+                rhs_scale=moving[1][:, moving_cols],
                 start=start,
                 stop=stop,
             )
 
-        def dh(n):
+        def new_bank(key, tag):
+            bank[key] = psum.tile([P, 512], F32, name=tag, tag=tag, bufs=BANKS[tag])
+            return bank[key]
+
+        def product_dh(n):
             f, g = UNITS[n]
-            for j in range(4):
-                dhb[n, j] = psum.tile([P, 512], F32, name="dh", tag="dh", bufs=4)
-                mx(dhb[n, j], g_c, g_s, g * 512 + j * 128, E5, w2_c, w2_s, f * 512, E4, True, True)
+            for s in range(4):
+                mx_pass(new_bank(("dh", n, s), "dh"), g_mx, g * 512 + s * P, E5M2, w2_mx, f * 512, E4M3, True, True)
+
+        def product_dp(g, uv, tag):
+            out = new_bank(("dp", g, uv), tag)
+            for f in range(2):
+                mx_pass(
+                    out, w1_mx, f * PATCH + uv * P, E4M3, hid_mx, f * TOKENS + g * 512, E5M2, f == 0, f == 1
+                )
+
+        def product_out_1(f, block, groups, tag):
+            out = new_bank(("out_1", f, block), tag) if groups[0] == 0 else bank["out_1", f, block]
+            for g in groups:
+                mx_pass(
+                    out,
+                    tok_mx,
+                    g * HIDDEN + f * 512 + block * P,
+                    E5M2,
+                    p_mx,
+                    g * PATCH,
+                    E4M3,
+                    g == 0,
+                    g == GROUPS - 1,
+                )
 
         def silu(n):
-            rt[n] = rot.tile([P, 4, 512], F32, name="rt", tag="rt", bufs=2)
-            for j in (0, 2):
+            factor[n] = rot.tile([P, 4, 512], F32, name="factor", tag="factor", bufs=2)
+            for s in (0, 2):
                 nc.scalar.activation(
-                    out=rt[n][:, j : j + 2, :], in_=o1t[n][:, j : j + 2, :], func=ACT.Silu, scale=-1.0
+                    out=factor[n][:, s : s + 2, :], in_=tanh_o1[n][:, s : s + 2, :], func=ACT.Silu, scale=-1.0
                 )
 
         def tanh(n):
-            for j in (0, 2):
+            for s in (0, 2):
                 nc.scalar.activation(
-                    out=o1t[n][:, j : j + 2, :], in_=o1t[n][:, j : j + 2, :], func=ACT.Tanh, scale=0.5
+                    out=tanh_o1[n][:, s : s + 2, :], in_=tanh_o1[n][:, s : s + 2, :], func=ACT.Tanh, scale=0.5
                 )
 
-        def d1(n):
-            for j in range(4):
+        def scale_dh(n):
+            for s in range(4):
                 nc.vector.scalar_tensor_tensor(
-                    out=rt[n][:, j, :],
-                    in0=rt[n][:, j, :],
+                    out=factor[n][:, s, :],
+                    in0=factor[n][:, s, :],
                     scalar=1.0,
-                    in1=dhb[n, j][:],
+                    in1=bank["dh", n, s][:],
                     op0=ALU.subtract,
                     op1=ALU.mult,
                 )
 
-        def d2(n):
-            dzn[n] = rot.tile([P, 4, 512], BF16, name="dzn", tag="dzn", bufs=2)
+        def make_dz(n):
+            dz[n] = rot.tile([P, 4, 512], BF16, name="dz", tag="dz", bufs=2)
             nc.vector.scalar_tensor_tensor(
-                out=dzn[n][:], in0=o1t[n][:], scalar=1.0, in1=rt[n][:], op0=ALU.add, op1=ALU.mult
+                out=dz[n][:], in0=tanh_o1[n][:], scalar=1.0, in1=factor[n][:], op0=ALU.add, op1=ALU.mult
             )
 
-        def mix_dz(n):
-            dzi[n] = rot.tile([P, 2048], BF16, name="dzi", tag="dzi", bufs=2, align_bytes=64)
-            nc.vector.tensor_copy(
-                out=dzi[n][:].rearrange("p (m t j) -> p m j t", t=4, j=4),
-                in_=dzn[n][:].rearrange("p j (m t) -> p m j t", t=4),
-            )
-
-        def tr(n):
-            for b in range(2):
-                bank = psum.tile([P, 4, P], F32, name="tr", tag="tr", bufs=2)
-                trb[n, b] = bank
+        def transpose_dz(n):
+            for pair in range(2):
+                out = psum.tile([P, 4, P], F32, name="tr", tag="tr", bufs=BANKS["tr"])
+                bank["tr", n, pair] = out
                 for k in range(4):
-                    words = dzn[n][:, 2 * b + k // 2, :].bitcast(F32)
-                    nc.tensor.transpose(bank[:, k, :], words[:, k % 2 : 256 : 2], idf[:])
+                    words = dz[n][:, 2 * pair + k // 2, :].bitcast(F32)
+                    nc.tensor.transpose(out[:, k, :], words[:, k % 2 : 256 : 2], ident_f32[:])
 
-        def cp_tr(n):
-            hidi[n] = rot.tile([P, 2048], BF16, name="hidi", tag="hidi", bufs=2, align_bytes=64)
-            words = hidi[n][:].bitcast(F32).rearrange("m (p b k) -> m b p k", b=2, k=4)
-            for b in range(2):
-                nc.scalar.copy(out=words[:, b], in_=trb[n, b][:].rearrange("m k p -> m p k"))
+        def copy_dz(n):
+            mixed["hid", n] = rot.tile([P, 2048], BF16, name="hid", tag="hid", bufs=2, align_bytes=64)
+            words = mixed["hid", n][:].bitcast(F32).rearrange("m (p pair k) -> m pair p k", pair=2, k=4)
+            for pair in range(2):
+                nc.scalar.copy(out=words[:, pair], in_=bank["tr", n, pair][:].rearrange("m k p -> m p k"))
 
         def sort_x(g):
-            xsb[g] = rot.tile([P, 2, 4, P], F32, name="xs", tag="xs", bufs=1)
-            words = xraw[g][:].bitcast(F32).rearrange("c (i u j t) -> c u i j t", i=16, u=2, t=4)
+            x_sorted[g] = rot.tile([P, 2, 4, P], F32, name="x_sorted", tag="x_sorted", bufs=1)
+            words = x_raw[g][:].bitcast(F32).rearrange("c (i u j t) -> c u i j t", i=16, u=2, t=4)
             for u in range(2):
                 nc.vector.tensor_copy(
-                    out=xsb[g][:, u, :, :].rearrange("c t (i j) -> c i j t", i=16), in_=words[:, u]
+                    out=x_sorted[g][:, u, :, :].rearrange("c t (i j) -> c i j t", i=16), in_=words[:, u]
                 )
 
-        def tr_x(g):
+        def transpose_x(g):
             for u in range(2):
-                bank = psum.tile([P, 4, P], F32, name="acc", tag="acc", bufs=2)
-                trb["x", g, u] = bank
+                out = psum.tile([P, 4, P], F32, name="acc", tag="acc", bufs=BANKS["acc"])
+                bank["x", g, u] = out
                 for t in range(4):
-                    nc.tensor.transpose(bank[:, t, :], xsb[g][:, u, t, :], idf[:])
+                    nc.tensor.transpose(out[:, t, :], x_sorted[g][:, u, t, :], ident_f32[:])
 
-        def cp_x(g):
-            d = mix_tile(("p", g))
+        def copy_x(g):
+            dst = new_mix(("p", g))
             for u in range(2):
+                src = bank["x", g, u][:].rearrange("p t c -> p (t c)").bitcast(BF16)
                 nc.scalar.copy(
-                    out=d[:, 1024 * u : 1024 * (u + 1)].rearrange("m (c t) -> m c t", t=4),
-                    in_=trb["x", g, u][:].rearrange("m t p -> m (t p)").bitcast(BF16).rearrange("m (t c) -> m c t", t=4),
+                    out=dst[:, 1024 * u : 1024 * (u + 1)].rearrange("p (cv t) -> p cv t", t=4),
+                    in_=src.rearrange("p (t cv) -> p cv t", t=4),
                 )
 
-        def pool_mm(g):
-            accb["p", g] = psum.tile([P, 512], F32, name="acc", tag="acc", bufs=2)
-            for j in range(4):
-                nc.tensor.matmul(
-                    accb["p", g][:], lhsT=idb[:], rhs=graw[g][:, j, :], start=(j == 0), stop=(j == 3)
-                )
+        def pool(g):
+            out = new_bank(("pool", g), "acc")
+            for s in range(4):
+                nc.tensor.matmul(out[:], lhsT=ident_bf16[:], rhs=g_raw[g][:, s, :], start=(s == 0), stop=(s == 3))
 
-        def cp_pool(g):
-            nc.scalar.copy(out=pooled[:, g * 512 : (g + 1) * 512], in_=accb["p", g][:])
+        def copy_pool(g):
+            nc.scalar.copy(out=pooled[:, g * 512 : (g + 1) * 512], in_=bank["pool", g][:])
 
-        def dps(g, q, tag="acc"):
-            accb[g, q] = psum.tile([P, 512], F32, name=tag, tag=tag, bufs=BUFS[tag])
-            for f in range(2):
-                mx(accb[g, q], w1_c, w1_s, f * 512 + q * 128, E4, hid_c, hid_s, f * T + g * 512, E5, f == 0, f == 1)
-
-        def stage(g, q, on_vector=False):
-            u, v = divmod(q, 2)
+        def stage_dp(g, uv):
+            u, v = divmod(uv, 2)
             if v == 0:
-                stg[g, u] = rot.tile([P, 2, 512], F32, name="stg", tag="stg", bufs=3)
-            copy = nc.vector.tensor_copy if on_vector else nc.scalar.copy
-            copy(out=stg[g, u][:, v, :], in_=accb[g, q][:])
+                staged[g, u] = rot.tile([P, 2, 512], F32, name="staged", tag="staged", bufs=4)
+            nc.scalar.copy(out=staged[g, u][:, v, :], in_=bank["dp", g, uv][:])
 
-        def add(g, u, h):
+        def add_pooled(g, u, quarter):
             if u == 0:
-                accb[g, h, "o"] = rot.tile([P, 1024], F32, name="o0t", tag="o0t", bufs=3)
-            o = accb[g, h, "o"]
-            src = stg[g, u][:, :, h * 256 : h * 256 + 256]
-            pl = pooled[:, g * 512 + h * 256 : g * 512 + h * 256 + 256]
+                pixels[g, quarter] = rot.tile([P, 1024], F32, name="pixels", tag="pixels", bufs=4)
+            out = pixels[g, quarter]
+            tokens = pooled[:, g * 512 + quarter * 256 : g * 512 + quarter * 256 + 256]
             nc.vector.scalar_tensor_tensor(
-                out=o[:].rearrange("c (i u j v) -> c u i j v", u=2, j=32, v=2)[:, u],
-                in0=pl.rearrange("c (i j) -> c i j", j=32).unsqueeze(3).to_broadcast([P, 8, 32, 2]),
+                out=out[:].rearrange("c (i u j v) -> c u i j v", u=2, j=32, v=2)[:, u],
+                in0=tokens.rearrange("c (i j) -> c i j", j=32).unsqueeze(3).to_broadcast([P, 8, 32, 2]),
                 scalar=0.25,
-                in1=src.rearrange("c v (i j) -> c i j v", j=32),
+                in1=staged[g, u][:, :, quarter * 256 : quarter * 256 + 256].rearrange("c v (i j) -> c i j v", j=32),
                 op0=ALU.mult,
                 op1=ALU.add,
             )
             if u == 1:
-                b, s = divmod(g, 2)
-                nc.sync.dma_start(out=o0v[b, s, :, h * 1024 : h * 1024 + 1024], in_=o[:])
+                image, part = divmod(g, 2)
+                nc.sync.dma_start(out=out_0_hbm[image, part, :, quarter * 1024 : quarter * 1024 + 1024], in_=out[:])
 
-        def dw1(f, t, gs, tag):
-            if gs[0] == 0:
-                accb["w", f, t] = psum.tile([P, 512], F32, name=tag, tag=tag, bufs=BUFS[tag])
-            for g in gs:
-                mx(accb["w", f, t], tok_c, tok_s, g * HID + f * 512 + t * 128, E5, p_c, p_s, g * 512, E4, g == 0, g == 3)
-
-        def out1(f, t, on_vector):
-            res = rot.tile([P, 512], F32, name="res", tag="res", bufs=4)
-            dst = res[:].rearrange("m (c u v) -> m c u v", u=2, v=2)
-            src = accb["w", f, t][:].rearrange("m (u c v) -> m c u v", u=2, v=2)
-            if on_vector:
-                nc.vector.tensor_copy(out=dst, in_=src)
-            else:
-                nc.scalar.copy(out=dst, in_=src)
-            nc.sync.dma_start(out=o1o[f, t], in_=res[:])
+        def store_out_1(f, block, copy):
+            rows = rot.tile([P, 512], F32, name="rows", tag="rows", bufs=4)
+            copy(
+                out=rows[:].rearrange("m (c u v) -> m c u v", u=2, v=2),
+                in_=bank["out_1", f, block][:].rearrange("m (u c v) -> m c u v", u=2, v=2),
+            )
+            nc.sync.dma_start(out=out_1_hbm[f, block], in_=rows[:])
 
         with tc.manual_schedule():
             load_g(0)
-            load_w(2, 0)
+            load_w2(0)
             load_o1(0)
             load_g(1)
             load_o1(1)
+            load_w2(1)
             load_g(2)
             load_x(0)
-            load_w(2, 1)
-            load_o1(2)
             load_g(3)
+            load_o1(2)
             load_x(1)
             load_o1(3)
 
@@ -310,113 +358,126 @@ def tile_memoryefficientpatchdownscale_v_kernel(
             mix_w2(0)
             q_g(0)
             q_w2(0)
-            pool_mm(0)
-            dh(0)
+            pool(0)
+            product_dh(0)
             silu(0)
             tanh(0)
-            cp_pool(0)
+            copy_pool(0)
 
-            for n in range(NU):
-                last = n == NU - 1
-                if 1 <= n <= G:
-                    tr_x(n - 1)
-                    cp_x(n - 1)
-                d1(n)
+            for n in range(len(UNITS)):
+                if 1 <= n <= GROUPS:
+                    transpose_x(n - 1)
+                    copy_x(n - 1)
+
+                if n == 1:
+                    q_tok(0)
+                    gpsimd_mix_g(3)
+                if n == 2:
+                    q_g(3)
+                if n >= 3:
+                    q_tok(n - 2)
+                if n >= 2:
+                    gpsimd_mix_dz(n - 1)
+                if n == 5:
+                    for uv in (0, 1):
+                        product_dp(0, uv, "acc")
+                        stage_dp(0, uv)
+                scale_dh(n)
+
                 if n == 0:
                     mix_g(1)
                 if n >= 6:
                     q_hid(n - 1)
                 if n == 1:
                     q_g(2)
+                    rest_mix_g(3)
                 if n == 2:
                     q_w2(1)
-                if n == 3:
-                    q_g(3)
                 if n == 4:
                     q_w1(0)
-                if n == 5:
-                    q_w1(1)
-                if not last and n > 0:
-                    dh(n + 1)
+                if 0 < n < LAST:
+                    product_dh(n + 1)
                     silu(n + 1)
-                if last:
-                    dw1(1, 0, range(2), "dh")
-                    dw1(1, 1, range(2), "dh")
-                if 5 <= n:
-                    for q in range(4):
-                        dps(n - 5, q)
-                        stage(n - 5, q)
-                d2(n)
+                if n == LAST:
+                    for block in (2, 3):
+                        product_out_1(0, block, range(GROUPS), "dh")
+                        store_out_1(0, block, nc.scalar.copy)
+                if n >= 5:
+                    for uv in range(2 if n == 5 else 0, 4):
+                        product_dp(n - 5, uv, "dh" if n == LAST and uv >= 2 else "acc")
+                        stage_dp(n - 5, uv)
+                if n >= 2:
+                    rest_mix_dz(n - 1)
+                make_dz(n)
+
                 if n == 0:
                     q_g(1)
-                    dh(1)
+                    product_dh(1)
                     silu(1)
-                if not last:
+                if n < LAST:
                     tanh(n + 1)
-                tr(n)
-                cp_tr(n)
-                if n > 0:
-                    q_tok(n - 1)
-                mix_dz(n)
-                if n + 4 < NU:
-                    load_o1(n + 4)
-                if n == 0:
-                    load_w(1, 0)
-                if n == 1:
-                    load_w(1, 1)
-                if n in (1, 2):
-                    load_x(n + 1)
-                if 1 <= n <= 5:
-                    q_hid(n - 1)
-                if 1 <= n <= G:
-                    q_p(n - 1)
-                if n == 0:
-                    mix_g(2)
-                if n == 1:
-                    mix_g(3)
-                if n < G:
-                    sort_x(n)
-                if 5 <= n:
-                    add(n - 5, 0, 0)
-                if last:
-                    q_tok(n)
-                    q_hid(n)
-                if 5 <= n:
-                    add(n - 5, 1, 0)
-                if 5 <= n and not last:
-                    add(n - 5, 0, 1)
-                    add(n - 5, 1, 1)
-                if n + 1 < G:
-                    pool_mm(n + 1)
-                    cp_pool(n + 1)
                 if n == 0:
                     mix_w2(1)
+                transpose_dz(n)
+                copy_dz(n)
+                if n == LAST:
+                    q_tok(n - 1)
+                if n in (0, LAST):
+                    mix_dz(n)
+
+                if n in (1, 2):
+                    load_x(n + 1)
+                if n in (0, 1):
+                    load_w1(n)
+                if n + 4 <= LAST:
+                    load_o1(n + 4)
+
+                if 1 <= n <= 5:
+                    q_hid(n - 1)
+                if 2 <= n <= 5:
+                    q_p(n - 2)
+                if n == 4:
+                    q_w1(1)
+                if n == 0:
+                    mix_g(2)
+                if n < GROUPS:
+                    sort_x(n)
+                if n >= 5:
+                    add_pooled(n - 5, 0, 0)
+                if n == LAST:
+                    q_hid(n)
+                    q_tok(n)
+                if n >= 5:
+                    add_pooled(n - 5, 0, 1)
+                if 5 <= n < LAST:
+                    add_pooled(n - 5, 1, 0)
+                    add_pooled(n - 5, 1, 1)
+                if n + 1 < GROUPS:
+                    pool(n + 1)
+                    copy_pool(n + 1)
                 if n in (2, 3):
                     mix_w1(n - 2)
-                if n in (5, 6):
-                    for t in (2 * n - 10, 2 * n - 9):
-                        dw1(0, t, range(G), "acc")
-                        out1(0, t, False)
-            for t in (2, 3):
-                dw1(1, t, (0, 1), "dh")
-            for t in (0, 1):
-                dw1(1, t, (2, 3), "dh")
-            dps(3, 0)
-            dps(3, 1)
-            dps(3, 2, "tr")
-            dps(3, 3, "tr")
-            for t in (2, 3):
-                dw1(1, t, (2, 3), "dh")
-            add(2, 0, 1)
-            add(2, 1, 1)
-            out1(1, 0, False)
-            out1(1, 1, True)
-            stage(3, 0)
-            stage(3, 1, True)
-            stage(3, 2)
-            stage(3, 3)
-            for h in range(2):
-                for u in range(2):
-                    add(3, u, h)
-            out1(1, 2, False)
-            out1(1, 3, False)
+                if n == 6:
+                    for block in (0, 1):
+                        product_out_1(0, block, range(GROUPS), "acc")
+                        store_out_1(0, block, nc.scalar.copy)
+
+            for block in (0, 1):
+                product_out_1(1, block, (0, 1), "dh")
+            for uv in range(4):
+                product_dp(3, uv, "acc" if uv < 2 else "dh")
+                stage_dp(3, uv)
+            for block in (0, 1):
+                product_out_1(1, block, (2, 3), "dh")
+            for block in (2, 3):
+                product_out_1(1, block, range(GROUPS), "tr")
+            for quarter in range(2):
+                add_pooled(2, 1, quarter)
+            for quarter in range(2):
+                add_pooled(3, 0, quarter)
+            store_out_1(1, 0, nc.scalar.copy)
+            store_out_1(1, 1, nc.scalar.copy)
+            add_pooled(3, 1, 0)
+            store_out_1(1, 2, nc.scalar.copy)
+            add_pooled(3, 1, 1)
+            store_out_1(1, 3, nc.vector.tensor_copy)

from contextlib import ExitStack

import concourse.mybir as mybir
from concourse.masks import make_identity

BATCH, CHANNELS, SIDE = 2, 128, 64
HIDDEN, OUT_CHANNELS, PATCH = 1024, 512, 512
TOKENS = 2048
P = 128
PASS = 512
GROUPS = TOKENS // PASS

F32 = mybir.dt.float32
BF16 = mybir.dt.bfloat16
U32 = mybir.dt.uint32
U8 = mybir.dt.uint8
E4M3 = mybir.dt.float8_e4m3fn_x4
E5M2 = mybir.dt.float8_e5m2_x4
ALU = mybir.AluOpType
ACT = mybir.ActivationFunctionType

FLOPS = 2 * TOKENS * HIDDEN * (OUT_CHANNELS + PATCH + PATCH)
BYTES = 2 * (BATCH * CHANNELS * SIDE * SIDE + HIDDEN * PATCH + OUT_CHANNELS * HIDDEN + TOKENS * OUT_CHANNELS) + 4 * (
    TOKENS * HIDDEN + BATCH * CHANNELS * SIDE * SIDE + HIDDEN * PATCH
)

UNITS = ((0, 0), (0, 1), (0, 2), (1, 0), (0, 3), (1, 1), (1, 2), (1, 3))
LAST = len(UNITS) - 1

BANKS = {"dh": 4, "tr": 2, "acc": 2}

W2_ON_SCALAR = (64, 128)

GPSIMD_COLUMNS = 384


def tile_memoryefficientpatchdownscale_v_kernel(
    tc, x, weight1, bias1, weight2, bias2, o1, grad_out, out_0, out_1
):
    nc = tc.nc

    g_hbm = grad_out.rearrange("b (p s) y w -> b p s (y w)", s=4)
    w2_hbm = weight2.rearrange("(p s) h -> p s h", s=4)
    w1_hbm = weight1.rearrange("(f p s) k -> f p s k", p=P, s=4)
    o1_hbm = o1.rearrange("(g p s) h -> g p s h", p=P, s=4)
    x_hbm = x.rearrange("b c (part r) w -> b part c (r w)", part=2)
    out_0_hbm = out_0.rearrange("b c (part r) w -> b part c (r w)", part=2)
    out_1_hbm = out_1.rearrange("(f block m) k -> f block m k", m=P, block=4)

    with ExitStack() as ctx:
        keep = ctx.enter_context(tc.tile_pool(name="keep", bufs=1))
        rot = ctx.enter_context(tc.tile_pool(name="rot", bufs=2))
        psum = ctx.enter_context(tc.psum_pool(name="psum", bufs=2))

        warm = keep.tile([P, 1], F32, name="warm")
        ident_f32 = keep.tile([P, P], F32, name="ident_f32")
        ident_bf16 = keep.tile([P, P], BF16, name="ident_bf16")
        pooled = keep.tile([P, TOKENS], F32, name="pooled")

        def mx_tiles(columns, name):
            codes = keep.tile([P, columns], U32, name=name + "_codes", align_bytes=64)
            scales = keep.tile([P, columns], U8, name=name + "_scales", align_bytes=64)
            return codes, scales

        g_mx = mx_tiles(TOKENS, "g")
        w2_mx = mx_tiles(HIDDEN, "w2")
        w1_mx = mx_tiles(2 * PATCH, "w1")
        p_mx = mx_tiles(GROUPS * PATCH, "p")
        tok_mx = mx_tiles(GROUPS * HIDDEN, "tok")
        hid_mx = mx_tiles(2 * TOKENS, "hid")

        nc.vector.memset(warm[:], 0.0)
        make_identity(nc, ident_f32[:])
        make_identity(nc, ident_bf16[:])

        g_raw, w_raw, x_raw, x_sorted = {}, {}, {}, {}
        mixed = {}
        tanh_o1, factor, dz = {}, {}, {}
        bank = {}
        staged, pixels = {}, {}

        def load_g(g):
            g_raw[g] = rot.tile([P, 4, 512], BF16, name="g_raw", tag="g_raw", bufs=4)
            image, part = divmod(g, 2)
            nc.sync.dma_start(out=g_raw[g][:], in_=g_hbm[image, :, :, part * 512 : (part + 1) * 512])

        def load_w2(f):
            w_raw["w2", f] = rot.tile([P, 4, 512], BF16, name="w_raw", tag="w_raw", bufs=3)
            nc.sync.dma_start(out=w_raw["w2", f][:], in_=w2_hbm[:, :, f * 512 : (f + 1) * 512])

        def load_w1(f):
            w_raw["w1", f] = rot.tile([P, 4, 512], BF16, name="w_raw", tag="w_raw", bufs=3)
            nc.sync.dma_start(out=w_raw["w1", f][:], in_=w1_hbm[f])

        def load_x(g):
            x_raw[g] = rot.tile([P, 2048], BF16, name="x_raw", tag="x_raw", bufs=2)
            image, part = divmod(g, 2)
            nc.sync.dma_start(out=x_raw[g][:], in_=x_hbm[image, part])

        def load_o1(n):
            f, g = UNITS[n]
            tanh_o1[n] = rot.tile([P, 4, 512], F32, name="o1t", tag="o1t", bufs=4)
            for s in (0, 2):
                nc.sync.dma_start(
                    out=tanh_o1[n][:, s : s + 2, :], in_=o1_hbm[g, :, s : s + 2, f * 512 : (f + 1) * 512]
                )

        def new_mix(key):
            mixed[key] = rot.tile([P, 2048], BF16, name="mix", tag="mix", bufs=3, align_bytes=64)
            return mixed[key]

        def new_gpsimd_mix(key):
            mixed[key] = rot.tile([P, 2048], BF16, name="mix_gp", tag="mix_gp", bufs=1, align_bytes=64)
            return mixed[key]

        def natural(tile):
            return tile.rearrange("p (m t s) -> p m s t", t=4, s=4)

        def permuted(tile):
            return tile.rearrange("p (t m s) -> p m s t", t=4, s=4)

        def by_slot(tile):
            return tile.rearrange("p s (m t) -> p m s t", t=4)

        def mix_g(g):
            nc.vector.tensor_copy(out=permuted(new_mix(("g", g))[:]), in_=by_slot(g_raw[g][:]))

        def mix_w1(f):
            nc.vector.tensor_copy(out=permuted(new_mix(("w1", f))[:]), in_=by_slot(w_raw["w1", f][:]))

        def mix_w2(f):
            dst, src = natural(new_mix(("w2", f))[:]), by_slot(w_raw["w2", f][:])
            cut = W2_ON_SCALAR[f]
            nc.scalar.mul(out=dst[:, :cut], in_=src[:, :cut], mul=-0.5)
            if cut < 128:
                nc.vector.tensor_scalar(out=dst[:, cut:], in0=src[:, cut:], scalar1=-0.5, scalar2=None, op0=ALU.mult)

        def gpsimd_copy(out, in_):
            nc.gpsimd.tensor_scalar(out=out, in0=in_, scalar1=1.0, scalar2=0.0, op0=ALU.mult, op1=ALU.add)

        def gpsimd_mix_g(g):
            quads = GPSIMD_COLUMNS // 4
            gpsimd_copy(
                new_gpsimd_mix(("g", g))[:].rearrange("p (t m s) -> p t m s", t=4, s=4)[:, :, :quads, :],
                g_raw[g][:].rearrange("p s (m t) -> p t m s", t=4)[:, :, :quads, :],
            )

        def rest_mix_g(g):
            quads = GPSIMD_COLUMNS // 4
            nc.vector.tensor_copy(out=permuted(mixed["g", g][:])[:, quads:], in_=by_slot(g_raw[g][:])[:, quads:])

        def mix_dz(n):
            nc.vector.tensor_copy(out=natural(new_gpsimd_mix(("tok", n))[:]), in_=by_slot(dz[n][:]))

        def gpsimd_mix_dz(n):
            gpsimd_copy(
                new_gpsimd_mix(("tok", n))[:, : 4 * GPSIMD_COLUMNS].rearrange("p (h s) -> p h s", s=4),
                dz[n][:, :, :GPSIMD_COLUMNS].rearrange("p s h -> p h s"),
            )

        def rest_mix_dz(n):
            nc.vector.tensor_copy(
                out=natural(mixed["tok", n][:, 4 * GPSIMD_COLUMNS :]), in_=by_slot(dz[n][:, :, GPSIMD_COLUMNS:])
            )

        def quantize(key, mx, column, fmt):
            codes, scales = mx
            cols = slice(column, column + 512)
            nc.vector.quantize_mx(out=codes[:, cols].bitcast(fmt), scales=scales[:, cols], in_=mixed[key][:])

        def q_g(g):
            quantize(("g", g), g_mx, g * 512, E5M2)

        def q_w2(f):
            quantize(("w2", f), w2_mx, f * 512, E4M3)

        def q_w1(f):
            quantize(("w1", f), w1_mx, f * PATCH, E4M3)

        def q_p(g):
            quantize(("p", g), p_mx, g * PATCH, E4M3)

        def q_tok(n):
            f, g = UNITS[n]
            quantize(("tok", n), tok_mx, g * HIDDEN + f * 512, E5M2)

        def q_hid(n):
            f, g = UNITS[n]
            quantize(("hid", n), hid_mx, f * TOKENS + g * 512, E5M2)

        def mx_pass(out, stationary, column, stationary_fmt, moving, moving_column, moving_fmt, start, stop):
            cols = slice(column, column + P)
            moving_cols = slice(moving_column, moving_column + PASS)
            nc.tensor.matmul_mx(
                out=out[:],
                lhsT=stationary[0][:, cols].bitcast(stationary_fmt),
                lhsT_scale=stationary[1][:, cols],
                rhs=moving[0][:, moving_cols].bitcast(moving_fmt),
                rhs_scale=moving[1][:, moving_cols],
                start=start,
                stop=stop,
            )

        def new_bank(key, tag):
            bank[key] = psum.tile([P, 512], F32, name=tag, tag=tag, bufs=BANKS[tag])
            return bank[key]

        def product_dh(n):
            f, g = UNITS[n]
            for s in range(4):
                mx_pass(new_bank(("dh", n, s), "dh"), g_mx, g * 512 + s * P, E5M2, w2_mx, f * 512, E4M3, True, True)

        def product_dp(g, uv, tag):
            out = new_bank(("dp", g, uv), tag)
            for f in range(2):
                mx_pass(
                    out, w1_mx, f * PATCH + uv * P, E4M3, hid_mx, f * TOKENS + g * 512, E5M2, f == 0, f == 1
                )

        def product_out_1(f, block, groups, tag):
            out = new_bank(("out_1", f, block), tag) if groups[0] == 0 else bank["out_1", f, block]
            for g in groups:
                mx_pass(
                    out,
                    tok_mx,
                    g * HIDDEN + f * 512 + block * P,
                    E5M2,
                    p_mx,
                    g * PATCH,
                    E4M3,
                    g == 0,
                    g == GROUPS - 1,
                )

        def silu(n):
            factor[n] = rot.tile([P, 4, 512], F32, name="factor", tag="factor", bufs=2)
            for s in (0, 2):
                nc.scalar.activation(
                    out=factor[n][:, s : s + 2, :], in_=tanh_o1[n][:, s : s + 2, :], func=ACT.Silu, scale=-1.0
                )

        def tanh(n):
            for s in (0, 2):
                nc.scalar.activation(
                    out=tanh_o1[n][:, s : s + 2, :], in_=tanh_o1[n][:, s : s + 2, :], func=ACT.Tanh, scale=0.5
                )

        def scale_dh(n):
            for s in range(4):
                nc.vector.scalar_tensor_tensor(
                    out=factor[n][:, s, :],
                    in0=factor[n][:, s, :],
                    scalar=1.0,
                    in1=bank["dh", n, s][:],
                    op0=ALU.subtract,
                    op1=ALU.mult,
                )

        def make_dz(n):
            dz[n] = rot.tile([P, 4, 512], BF16, name="dz", tag="dz", bufs=2)
            nc.vector.scalar_tensor_tensor(
                out=dz[n][:], in0=tanh_o1[n][:], scalar=1.0, in1=factor[n][:], op0=ALU.add, op1=ALU.mult
            )

        def transpose_dz(n):
            for pair in range(2):
                out = psum.tile([P, 4, P], F32, name="tr", tag="tr", bufs=BANKS["tr"])
                bank["tr", n, pair] = out
                for k in range(4):
                    words = dz[n][:, 2 * pair + k // 2, :].bitcast(F32)
                    nc.tensor.transpose(out[:, k, :], words[:, k % 2 : 256 : 2], ident_f32[:])

        def copy_dz(n):
            mixed["hid", n] = rot.tile([P, 2048], BF16, name="hid", tag="hid", bufs=2, align_bytes=64)
            words = mixed["hid", n][:].bitcast(F32).rearrange("m (p pair k) -> m pair p k", pair=2, k=4)
            for pair in range(2):
                nc.scalar.copy(out=words[:, pair], in_=bank["tr", n, pair][:].rearrange("m k p -> m p k"))

        def sort_x(g):
            x_sorted[g] = rot.tile([P, 2, 4, P], F32, name="x_sorted", tag="x_sorted", bufs=1)
            words = x_raw[g][:].bitcast(F32).rearrange("c (i u j t) -> c u i j t", i=16, u=2, t=4)
            for u in range(2):
                nc.vector.tensor_copy(
                    out=x_sorted[g][:, u, :, :].rearrange("c t (i j) -> c i j t", i=16), in_=words[:, u]
                )

        def transpose_x(g):
            for u in range(2):
                out = psum.tile([P, 4, P], F32, name="acc", tag="acc", bufs=BANKS["acc"])
                bank["x", g, u] = out
                for t in range(4):
                    nc.tensor.transpose(out[:, t, :], x_sorted[g][:, u, t, :], ident_f32[:])

        def copy_x(g):
            dst = new_mix(("p", g))
            for u in range(2):
                src = bank["x", g, u][:].rearrange("p t c -> p (t c)").bitcast(BF16)
                nc.scalar.copy(
                    out=dst[:, 1024 * u : 1024 * (u + 1)].rearrange("p (cv t) -> p cv t", t=4),
                    in_=src.rearrange("p (t cv) -> p cv t", t=4),
                )

        def pool(g):
            out = new_bank(("pool", g), "acc")
            for s in range(4):
                nc.tensor.matmul(out[:], lhsT=ident_bf16[:], rhs=g_raw[g][:, s, :], start=(s == 0), stop=(s == 3))

        def copy_pool(g):
            nc.scalar.copy(out=pooled[:, g * 512 : (g + 1) * 512], in_=bank["pool", g][:])

        def stage_dp(g, uv):
            u, v = divmod(uv, 2)
            if v == 0:
                staged[g, u] = rot.tile([P, 2, 512], F32, name="staged", tag="staged", bufs=4)
            nc.scalar.copy(out=staged[g, u][:, v, :], in_=bank["dp", g, uv][:])

        def add_pooled(g, u, quarter):
            if u == 0:
                pixels[g, quarter] = rot.tile([P, 1024], F32, name="pixels", tag="pixels", bufs=4)
            out = pixels[g, quarter]
            tokens = pooled[:, g * 512 + quarter * 256 : g * 512 + quarter * 256 + 256]
            nc.vector.scalar_tensor_tensor(
                out=out[:].rearrange("c (i u j v) -> c u i j v", u=2, j=32, v=2)[:, u],
                in0=tokens.rearrange("c (i j) -> c i j", j=32).unsqueeze(3).to_broadcast([P, 8, 32, 2]),
                scalar=0.25,
                in1=staged[g, u][:, :, quarter * 256 : quarter * 256 + 256].rearrange("c v (i j) -> c i j v", j=32),
                op0=ALU.mult,
                op1=ALU.add,
            )
            if u == 1:
                image, part = divmod(g, 2)
                nc.sync.dma_start(out=out_0_hbm[image, part, :, quarter * 1024 : quarter * 1024 + 1024], in_=out[:])

        def store_out_1(f, block, copy):
            rows = rot.tile([P, 512], F32, name="rows", tag="rows", bufs=4)
            copy(
                out=rows[:].rearrange("m (c u v) -> m c u v", u=2, v=2),
                in_=bank["out_1", f, block][:].rearrange("m (u c v) -> m c u v", u=2, v=2),
            )
            nc.sync.dma_start(out=out_1_hbm[f, block], in_=rows[:])

        with tc.manual_schedule():
            load_g(0)
            load_w2(0)
            load_o1(0)
            load_g(1)
            load_o1(1)
            load_w2(1)
            load_g(2)
            load_x(0)
            load_g(3)
            load_o1(2)
            load_x(1)
            load_o1(3)

            nc.scalar.activation(out=warm[:], in_=warm[:], func=ACT.Silu, scale=-1.0)
            mix_g(0)
            mix_w2(0)
            q_g(0)
            q_w2(0)
            pool(0)
            product_dh(0)
            silu(0)
            tanh(0)
            copy_pool(0)

            for n in range(len(UNITS)):
                if 1 <= n <= GROUPS:
                    transpose_x(n - 1)
                    copy_x(n - 1)

                if n == 1:
                    q_tok(0)
                    gpsimd_mix_g(3)
                if n == 2:
                    q_g(3)
                if n >= 3:
                    q_tok(n - 2)
                if n >= 2:
                    gpsimd_mix_dz(n - 1)
                if n == 5:
                    for uv in (0, 1):
                        product_dp(0, uv, "acc")
                        stage_dp(0, uv)
                scale_dh(n)

                if n == 0:
                    mix_g(1)
                if n >= 6:
                    q_hid(n - 1)
                if n == 1:
                    q_g(2)
                    rest_mix_g(3)
                if n == 2:
                    q_w2(1)
                if n == 4:
                    q_w1(0)
                if 0 < n < LAST:
                    product_dh(n + 1)
                    silu(n + 1)
                if n == LAST:
                    for block in (2, 3):
                        product_out_1(0, block, range(GROUPS), "dh")
                        store_out_1(0, block, nc.scalar.copy)
                if n >= 5:
                    for uv in range(2 if n == 5 else 0, 4):
                        product_dp(n - 5, uv, "dh" if n == LAST and uv >= 2 else "acc")
                        stage_dp(n - 5, uv)
                if n >= 2:
                    rest_mix_dz(n - 1)
                make_dz(n)

                if n == 0:
                    q_g(1)
                    product_dh(1)
                    silu(1)
                if n < LAST:
                    tanh(n + 1)
                if n == 0:
                    mix_w2(1)
                transpose_dz(n)
                copy_dz(n)
                if n == LAST:
                    q_tok(n - 1)
                if n in (0, LAST):
                    mix_dz(n)

                if n in (1, 2):
                    load_x(n + 1)
                if n in (0, 1):
                    load_w1(n)
                if n + 4 <= LAST:
                    load_o1(n + 4)

                if 1 <= n <= 5:
                    q_hid(n - 1)
                if 2 <= n <= 5:
                    q_p(n - 2)
                if n == 4:
                    q_w1(1)
                if n == 0:
                    mix_g(2)
                if n < GROUPS:
                    sort_x(n)
                if n >= 5:
                    add_pooled(n - 5, 0, 0)
                if n == LAST:
                    q_hid(n)
                    q_tok(n)
                if n >= 5:
                    add_pooled(n - 5, 0, 1)
                if 5 <= n < LAST:
                    add_pooled(n - 5, 1, 0)
                    add_pooled(n - 5, 1, 1)
                if n + 1 < GROUPS:
                    pool(n + 1)
                    copy_pool(n + 1)
                if n in (2, 3):
                    mix_w1(n - 2)
                if n == 6:
                    for block in (0, 1):
                        product_out_1(0, block, range(GROUPS), "acc")
                        store_out_1(0, block, nc.scalar.copy)

            for block in (0, 1):
                product_out_1(1, block, (0, 1), "dh")
            for uv in range(4):
                product_dp(3, uv, "acc" if uv < 2 else "dh")
                stage_dp(3, uv)
            for block in (0, 1):
                product_out_1(1, block, (2, 3), "dh")
            for block in (2, 3):
                product_out_1(1, block, range(GROUPS), "tr")
            for quarter in range(2):
                add_pooled(2, 1, quarter)
            for quarter in range(2):
                add_pooled(3, 0, quarter)
            store_out_1(1, 0, nc.scalar.copy)
            store_out_1(1, 1, nc.scalar.copy)
            add_pooled(3, 1, 0)
            store_out_1(1, 2, nc.scalar.copy)
            add_pooled(3, 1, 1)
            store_out_1(1, 3, nc.vector.tensor_copy)
